import numpy as np
import ml_dtypes


def mxq(x, axis, fmt="e4m3"):
    dtype, down = {"e4m3": (ml_dtypes.float8_e4m3fn, 7), "e5m2": (ml_dtypes.float8_e5m2, 14)}[fmt]
    v = np.moveaxis(np.asarray(x, np.float32).astype(ml_dtypes.bfloat16).astype(np.float64), axis, -1)
    blocks = v.reshape(v.shape[:-1] + (-1, 32))
    amax = np.abs(blocks).max(-1, keepdims=True)
    byte = np.maximum(np.where(amax > 0, np.frexp(amax)[1] - 1 + 127, 0) - down, 1)
    scale = np.exp2(byte - 127.0)
    codes = (blocks / scale).astype(np.float32).astype(dtype).astype(np.float64)
    return np.moveaxis((codes * scale).reshape(v.shape), -1, axis)


WIDE = False


def mx_kscale(k):
    if not WIDE:
        return np.ones(k)
    levels = np.array([10, -10, 5, -5, 0])
    a = np.random.permutation(np.resize(levels, k // 512 * 4)).reshape(k // 512, 4)
    idx = np.arange(k)
    return np.exp2(a[idx // 512, idx % 128 // 32])


BF16 = ml_dtypes.bfloat16


def bf(x):
    return np.asarray(x, np.float32).astype(BF16)


def f64(x):
    return np.asarray(x).astype(np.float64)


E2M1 = np.array([0.0, 0.5, 1.0, 1.5, 2.0, 3.0, 4.0, 6.0, -0.0, -0.5, -1.0, -1.5, -2.0, -3.0, -4.0, -6.0])


def pack_weight(w, fmt):
    k, n = w.shape
    w = f64(bf(w)).reshape(k // 32, 32, n)
    amax = np.abs(w).max(1)
    if fmt == "e4m3":
        byte = np.frexp(amax)[1] - 1 + 127 - 7
    else:
        mant, ex = np.frexp(amax / 6.0)
        byte = np.where(mant > 0.5, ex, ex - 1) + 127
    byte = np.clip(np.where(amax > 0, byte, 1), 1, 254)
    scaled = (w * np.exp2(127.0 - byte)[:, None, :]).reshape(k, n).astype(np.float32)
    by_word = np.ascontiguousarray(scaled.reshape(k // 512, 128, 4, n).transpose(0, 1, 3, 2))
    if fmt == "e4m3":
        words = by_word.astype(ml_dtypes.float8_e4m3fn).view(np.uint8)
    else:
        c = by_word.astype(ml_dtypes.float4_e2m1fn).view(np.uint8) & 0xF
        words = c[..., 0::2] | (c[..., 1::2] << 4)
    return np.ascontiguousarray(words), np.ascontiguousarray(byte.astype(np.uint8).reshape(k // 512, 16, n))


def unpack_weight(words, scales, fmt):
    g, p, n, _ = words.shape
    if fmt == "e4m3":
        vals = np.ascontiguousarray(words).view(ml_dtypes.float8_e4m3fn).astype(np.float64)
    else:
        nib = np.empty((g, p, n, 4), np.uint8)
        nib[..., 0::2] = words & 0xF
        nib[..., 1::2] = words >> 4
        vals = E2M1[nib]
    vals = vals * np.repeat(np.exp2(scales.astype(np.float64) - 127.0), 8, axis=1)[..., None]
    return vals.transpose(0, 1, 3, 2).reshape(g * 512, n)


B, M, D, N, P, H = 32, 1024, 512, 8, 16, 1024
R = B * P
FMT = "e4m3"


def silu(v):
    return v / (1.0 + np.exp(-v))


def setup_inputs():
    s = mx_kscale(D)
    xs_mix = bf(np.random.standard_normal((B, N, P, D)) * 0.3 / np.sqrt(D) * s)
    task_emb = bf(np.random.standard_normal((P, D)) * 0.5 / np.sqrt(D) * s)
    w1 = np.random.standard_normal((N, D, H)) * 2.0 / s[:, None]
    W1_words, W1_scales = pack_weight(w1.reshape(-1, H), FMT)
    b1 = bf(np.random.standard_normal((N, H)) * 0.3)
    w2 = np.random.standard_normal((N, H, D)) / np.sqrt(H * D) * s
    W2_words, W2_scales = pack_weight(w2.reshape(-1, D), FMT)
    b2 = bf(np.random.standard_normal((N, D)) * 0.3 / np.sqrt(D) * s)
    ln_g = bf(1.0 + 0.1 * np.random.standard_normal((N, D)))
    ln_b = bf(0.1 * np.random.standard_normal((N, D)))
    return {"xs_mix": xs_mix,
            "task_emb": task_emb,
            "W1_words": W1_words,
            "W1_scales": W1_scales,
            "b1": b1,
            "W2_words": W2_words,
            "W2_scales": W2_scales,
            "b2": b2,
            "ln_g": ln_g,
            "ln_b": ln_b}


def reference(xs_mix, task_emb, W1_words, W1_scales, b1, W2_words, W2_scales, b2, ln_g, ln_b):
    xs = f64(xs_mix) + f64(task_emb)[None, None, :, :]
    xe = xs.transpose(1, 0, 2, 3).reshape(N, R, D)
    h = silu((mxq(xe, 2, "e4m3") @ unpack_weight(W1_words, W1_scales, FMT).reshape(N, D, H)) + f64(b1)[:, None, :])
    mlp = (mxq(h, 2, "e4m3") @ unpack_weight(W2_words, W2_scales, FMT).reshape(N, H, D)) + f64(b2)[:, None, :]
    r = xe + mlp
    mu = r.mean(-1, keepdims=True)
    var = ((r - mu) ** 2).mean(-1, keepdims=True)
    ys = (r - mu) / np.sqrt(var + 1e-5) * f64(ln_g)[:, None, :] + f64(ln_b)[:, None, :]
    return ys.reshape(N, B, P, D).transpose(1, 0, 2, 3)

@@ -1,0 +1,274 @@
+from contextlib import ExitStack
+
+import concourse.mybir as mybir
+from concourse.masks import make_identity
+
+F32 = mybir.dt.float32
+BF16 = mybir.dt.bfloat16
+I32 = mybir.dt.int32
+U32 = mybir.dt.uint32
+U8 = mybir.dt.uint8
+FP8X4 = mybir.dt.float8_e4m3fn_x4
+ALU = mybir.AluOpType
+ACT = mybir.ActivationFunctionType
+
+P = 128
+PACK = 4
+K_PASS = P * PACK
+BATCH, EXPERTS, TASKS, D, H = 32, 8, 16, 512, 1024
+LN_EPS = 1e-5
+
+B_TILE = P // TASKS
+TILES_PER_EXPERT = BATCH // B_TILE
+N_TILES = EXPERTS * TILES_PER_EXPERT
+H_PASSES = H // K_PASS
+PLANES_PER_TILE = 4
+ROWS_AHEAD = 3
+
+FLOPS = 2 * BATCH * EXPERTS * TASKS * (D * H + H * D)
+
+
+def tile_hdmodel_pb_t_e_kernel(
+    tc, xs_mix, task_emb, W1_words, W1_scales, b1, W2_words, W2_scales, b2, ln_g, ln_b, out
+):
+    nc = tc.nc
+    with ExitStack() as ctx:
+        const = ctx.enter_context(tc.tile_pool(name="const", bufs=1))
+        expert_pool = ctx.enter_context(tc.tile_pool(name="expert", bufs=3))
+        rows_pool = ctx.enter_context(tc.tile_pool(name="rows", bufs=ROWS_AHEAD + 3))
+        xq_pool = ctx.enter_context(tc.tile_pool(name="xq", bufs=3))
+        hb_pool = ctx.enter_context(tc.tile_pool(name="hb", bufs=2 * H_PASSES))
+        hq_pool = ctx.enter_context(tc.tile_pool(name="hq", bufs=3))
+        resid_pool = ctx.enter_context(tc.tile_pool(name="resid", bufs=4))
+        ln_pool = ctx.enter_context(tc.tile_pool(name="ln", bufs=3))
+        stat_pool = ctx.enter_context(tc.tile_pool(name="stat", bufs=4))
+        psum_x = ctx.enter_context(tc.psum_pool(name="psum_x", bufs=1))
+        psum_h1 = ctx.enter_context(tc.psum_pool(name="psum_h1", bufs=2))
+        psum_ht = ctx.enter_context(tc.psum_pool(name="psum_ht", bufs=3))
+        psum_o = ctx.enter_context(tc.psum_pool(name="psum_o", bufs=2))
+
+        ident = const.tile([P, P], F32)
+        make_identity(nc, ident[:])
+        neg_half = const.tile([P, 1], F32)
+        nc.vector.memset(neg_half[:], -0.5)
+
+        w1_planes = const.tile([P, EXPERTS // PLANES_PER_TILE, H], U8, align_bytes=64)
+        w2_planes = const.tile([P, EXPERTS * H_PASSES // PLANES_PER_TILE, D], U8, align_bytes=64)
+        nc.vector.memset(w1_planes[:].rearrange("p b n -> p (b n)").bitcast(I32), 0)
+        nc.vector.memset(w2_planes[:].rearrange("p b n -> p (b n)").bitcast(I32), 0)
+
+        def load_planes(planes, scales, block):
+            first = PLANES_PER_TILE * block
+            for quadrant in range(4):
+                nc.sync.dma_start(
+                    out=planes[32 * quadrant : 32 * quadrant + 16, block, :].bitcast(I32),
+                    in_=scales[
+                        first : first + PLANES_PER_TILE, 4 * quadrant : 4 * quadrant + 4, :
+                    ].bitcast(I32),
+                )
+
+        def rows_to_columns(x_rows):
+            words = x_rows[:].bitcast(F32)
+            x_cols = psum_x.tile([P, 2, P], F32)
+            for u in range(2):
+                nc.tensor.transpose(x_cols[:, u, :], words[:, u : D // 2 : 2], ident[:])
+            return x_cols
+
+        te_rows = const.tile([P, D], BF16)
+        nc.sync.dma_start(
+            out=te_rows[:], in_=task_emb.unsqueeze(1).to_broadcast([TASKS, B_TILE, D])
+        )
+        te_psum = rows_to_columns(te_rows)
+        te_cols = const.tile([P, P, PACK], BF16)
+        nc.vector.tensor_copy(
+            out=te_cols[:].rearrange("p r t -> p (r t)").bitcast(F32).rearrange("p (r u) -> p r u", u=2),
+            in_=te_psum[:].rearrange("p u r -> p r u"),
+        )
+
+        experts = {}
+        tiles = {}
+
+        def load_expert(e):
+            if e % PLANES_PER_TILE == 0:
+                load_planes(w1_planes, W1_scales, e // PLANES_PER_TILE)
+            w1_words = expert_pool.tile([P, PACK * H], U8, align_bytes=64)
+            nc.sync.dma_start(
+                out=w1_words[:].bitcast(I32),
+                in_=W1_words[e].rearrange("p n t -> p (n t)").bitcast(I32),
+            )
+            b1_rows = expert_pool.tile([P, H], BF16)
+            nc.sync.dma_start(out=b1_rows[:], in_=b1[e].partition_broadcast(P))
+            if (e * H_PASSES) % PLANES_PER_TILE == 0:
+                load_planes(w2_planes, W2_scales, e * H_PASSES // PLANES_PER_TILE)
+            w2_words = expert_pool.tile([P, H_PASSES, PACK * D], U8, align_bytes=64)
+            for c in range(H_PASSES):
+                nc.sync.dma_start(
+                    out=w2_words[:, c, :].bitcast(I32),
+                    in_=W2_words[e * H_PASSES + c].rearrange("p n t -> p (n t)").bitcast(I32),
+                )
+            b2_rows = expert_pool.tile([P, D], BF16)
+            nc.sync.dma_start(out=b2_rows[:], in_=b2[e].partition_broadcast(P))
+            gain_rows = expert_pool.tile([P, D], BF16)
+            nc.sync.dma_start(out=gain_rows[:], in_=ln_g[e].partition_broadcast(P))
+            bias_rows = expert_pool.tile([P, D], BF16)
+            nc.sync.dma_start(out=bias_rows[:], in_=ln_b[e].partition_broadcast(P))
+            te_b2 = expert_pool.tile([P, D], F32)
+            nc.gpsimd.tensor_tensor(out=te_b2[:], in0=te_rows[:], in1=b2_rows[:], op=ALU.add)
+            experts[e] = dict(
+                w1_words=w1_words, b1_rows=b1_rows, w2_words=w2_words,
+                gain_rows=gain_rows, bias_rows=bias_rows, te_b2=te_b2,
+            )
+
+        def dram_rows(tensor, j):
+            e, i = divmod(j, TILES_PER_EXPERT)
+            return tensor[B_TILE * i : B_TILE * (i + 1), e].rearrange("b t d -> t b d")
+
+        def load_rows(j):
+            x_rows = rows_pool.tile([P, D], BF16)
+            nc.sync.dma_start(out=x_rows[:], in_=dram_rows(xs_mix, j))
+            tiles[j] = dict(x_rows=x_rows)
+
+        def stage_1_quantise_rows(j):
+            x_cols = rows_to_columns(tiles[j]["x_rows"])
+            x_grouped = xq_pool.tile([P, P, PACK], BF16, align_bytes=64)
+            nc.vector.tensor_tensor(
+                out=x_grouped[:].rearrange("p r (u e) -> p r u e", e=2),
+                in0=x_cols[:].bitcast(BF16).rearrange("p u (r e) -> p r u e", e=2),
+                in1=te_cols[:].rearrange("p r (u e) -> p r u e", e=2),
+                op=ALU.add,
+            )
+            x_codes = xq_pool.tile([P, P], U32, align_bytes=64)
+            x_scales = xq_pool.tile([P, P], U8, align_bytes=64)
+            nc.vector.quantize_mx(
+                out=x_codes[:].bitcast(FP8X4),
+                scales=x_scales[:],
+                in_=x_grouped[:].rearrange("p r t -> p (r t)"),
+            )
+            tiles[j]["x_codes"] = x_codes
+            tiles[j]["x_scales"] = x_scales
+
+        def stage_2_first_matmul(j):
+            e = j // TILES_PER_EXPERT
+            block, plane = divmod(e, PLANES_PER_TILE)
+            pre_act = []
+            for c in range(H_PASSES):
+                cols = slice(K_PASS * c, K_PASS * (c + 1))
+                h_psum = psum_h1.tile([P, K_PASS], F32)
+                nc.tensor.matmul_mx(
+                    out=h_psum[:],
+                    lhsT=tiles[j]["x_codes"][:].bitcast(FP8X4),
+                    lhsT_scale=tiles[j]["x_scales"][:],
+                    rhs=experts[e]["w1_words"][:, PACK * K_PASS * c : PACK * K_PASS * (c + 1)].bitcast(FP8X4),
+                    rhs_scale=w1_planes[4 * plane : P, block, cols],
+                    start=True,
+                    stop=True,
+                )
+                h_sorted = hb_pool.tile([P, PACK, P], F32)
+                nc.vector.tensor_tensor(
+                    out=h_sorted[:],
+                    in0=h_psum[:].rearrange("r (p t) -> r t p", t=PACK),
+                    in1=experts[e]["b1_rows"][:, cols].rearrange("r (p t) -> r t p", t=PACK),
+                    op=ALU.add,
+                )
+                pre_act.append(h_sorted)
+            resid = resid_pool.tile([P, D], F32)
+            nc.gpsimd.tensor_tensor(
+                out=resid[:], in0=tiles[j]["x_rows"][:], in1=experts[e]["te_b2"][:], op=ALU.add
+            )
+            tiles[j]["pre_act"] = pre_act
+            tiles[j]["resid"] = resid
+
+        def stage_3_quantise_hidden(j):
+            h_grouped = hq_pool.tile([P, H_PASSES, P, PACK], BF16, align_bytes=64)
+            for c in range(H_PASSES):
+                h_cols = psum_ht.tile([P, PACK, P], F32)
+                for t in range(PACK):
+                    nc.tensor.transpose(h_cols[:, t, :], tiles[j]["pre_act"][c][:, t, :], ident[:])
+                nc.scalar.activation(
+                    out=h_grouped[:, c, :, :],
+                    in_=h_cols[:].rearrange("p t r -> p r t"),
+                    func=ACT.Silu,
+                )
+            h_codes = hq_pool.tile([P, H_PASSES * P], U32, align_bytes=64)
+            h_scales = hq_pool.tile([P, H_PASSES * P], U8, align_bytes=64)
+            nc.vector.quantize_mx(
+                out=h_codes[:].bitcast(FP8X4),
+                scales=h_scales[:],
+                in_=h_grouped[:].rearrange("p c r t -> p (c r t)"),
+            )
+            tiles[j]["h_codes"] = h_codes
+            tiles[j]["h_scales"] = h_scales
+
+        def stage_4_second_matmul(j):
+            e = j // TILES_PER_EXPERT
+            o_psum = psum_o.tile([P, D], F32)
+            for c in range(H_PASSES):
+                block, plane = divmod(e * H_PASSES + c, PLANES_PER_TILE)
+                nc.tensor.matmul_mx(
+                    out=o_psum[:],
+                    lhsT=tiles[j]["h_codes"][:, P * c : P * (c + 1)].bitcast(FP8X4),
+                    lhsT_scale=tiles[j]["h_scales"][:, P * c : P * (c + 1)],
+                    rhs=experts[e]["w2_words"][:, c, :].bitcast(FP8X4),
+                    rhs_scale=w2_planes[4 * plane : P, block, :],
+                    start=(c == 0),
+                    stop=(c == H_PASSES - 1),
+                )
+            r = ln_pool.tile([P, D], F32)
+            r_sum = stat_pool.tile([P, 1], F32)
+            nc.vector.scalar_tensor_tensor(
+                out=r[:], in0=o_psum[:], scalar=1.0, in1=tiles[j]["resid"][:],
+                op0=ALU.mult, op1=ALU.add, accum_out=r_sum[:],
+            )
+            neg_mean = stat_pool.tile([P, 1], F32)
+            nc.gpsimd.tensor_scalar(
+                out=neg_mean[:], in0=r_sum[:], scalar1=-1.0 / D, scalar2=0.0, op0=ALU.mult, op1=ALU.add
+            )
+            squares = ln_pool.tile([P, D], BF16)
+            dev_sum = stat_pool.tile([P, 1], F32)
+            nc.scalar.activation(
+                out=squares[:], in_=r[:], func=ACT.Square, bias=neg_mean[:, 0:1], scale=1.0,
+                accum_out=dev_sum[:],
+            )
+            tiles[j]["r"] = r
+            tiles[j]["neg_mean"] = neg_mean
+            tiles[j]["dev_sum"] = dev_sum
+
+        def stage_5_layer_norm(j):
+            e = j // TILES_PER_EXPERT
+            var_eps = stat_pool.tile([P, 1], F32)
+            nc.gpsimd.tensor_scalar(
+                out=var_eps[:], in0=tiles[j]["dev_sum"][:], scalar1=1.0 / D, scalar2=LN_EPS,
+                op0=ALU.mult, op1=ALU.add,
+            )
+            rstd = stat_pool.tile([P, 1], F32)
+            nc.gpsimd.tensor_tensor(out=rstd[:], in0=var_eps[:], in1=neg_half[:], op=ALU.pow)
+            gained = ln_pool.tile([P, D], F32)
+            nc.vector.scalar_tensor_tensor(
+                out=gained[:], in0=tiles[j]["r"][:], scalar=tiles[j]["neg_mean"][:, 0:1],
+                in1=experts[e]["gain_rows"][:], op0=ALU.add, op1=ALU.mult,
+            )
+            scaled = ln_pool.tile([P, D], F32)
+            nc.scalar.activation(out=scaled[:], in_=gained[:], func=ACT.Copy, scale=rstd[:, 0:1])
+            y = ln_pool.tile([P, D], F32)
+            nc.gpsimd.tensor_tensor(out=y[:], in0=scaled[:], in1=experts[e]["bias_rows"][:], op=ALU.add)
+            nc.sync.dma_start(out=dram_rows(out, j), in_=y[:])
+
+        load_rows(0)
+        load_expert(0)
+        for j in range(1, ROWS_AHEAD):
+            load_rows(j)
+        for step in range(N_TILES + 4):
+            if step % TILES_PER_EXPERT == 0 and step // TILES_PER_EXPERT + 1 < EXPERTS:
+                load_expert(step // TILES_PER_EXPERT + 1)
+            if step + ROWS_AHEAD < N_TILES:
+                load_rows(step + ROWS_AHEAD)
+            if step < N_TILES:
+                stage_1_quantise_rows(step)
+            if 0 <= step - 2 < N_TILES:
+                stage_3_quantise_hidden(step - 2)
+            if 0 <= step - 1 < N_TILES:
+                stage_2_first_matmul(step - 1)
+            if 0 <= step - 3 < N_TILES:
+                stage_4_second_matmul(step - 3)
+            if 0 <= step - 4 < N_TILES:
+                stage_5_layer_norm(step - 4)

@@ -23,7 +23,8 @@ TILES_PER_EXPERT = BATCH // B_TILE
 N_TILES = EXPERTS * TILES_PER_EXPERT
 H_PASSES = H // K_PASS
 PLANES_PER_TILE = 4
-ROWS_AHEAD = 3
+ROWS_AHEAD = 5
+EXPERT_AHEAD = 6
 
 FLOPS = 2 * BATCH * EXPERTS * TASKS * (D * H + H * D)
 
@@ -33,29 +34,27 @@ def tile_hdmodel_pb_t_e_kernel(
 ):
     nc = tc.nc
     with ExitStack() as ctx:
+        ctx.enter_context(tc.manual_schedule())
         const = ctx.enter_context(tc.tile_pool(name="const", bufs=1))
         expert_pool = ctx.enter_context(tc.tile_pool(name="expert", bufs=3))
-        rows_pool = ctx.enter_context(tc.tile_pool(name="rows", bufs=ROWS_AHEAD + 3))
-        xq_pool = ctx.enter_context(tc.tile_pool(name="xq", bufs=3))
-        hb_pool = ctx.enter_context(tc.tile_pool(name="hb", bufs=2 * H_PASSES))
-        hq_pool = ctx.enter_context(tc.tile_pool(name="hq", bufs=3))
-        resid_pool = ctx.enter_context(tc.tile_pool(name="resid", bufs=4))
-        ln_pool = ctx.enter_context(tc.tile_pool(name="ln", bufs=3))
+        rows_pool = ctx.enter_context(tc.tile_pool(name="rows", bufs=ROWS_AHEAD + 2))
+        work = ctx.enter_context(tc.tile_pool(name="work", bufs=3))
+        sorted_pool = ctx.enter_context(tc.tile_pool(name="sorted", bufs=2 * H_PASSES))
         stat_pool = ctx.enter_context(tc.tile_pool(name="stat", bufs=4))
         psum_x = ctx.enter_context(tc.psum_pool(name="psum_x", bufs=1))
-        psum_h1 = ctx.enter_context(tc.psum_pool(name="psum_h1", bufs=2))
-        psum_ht = ctx.enter_context(tc.psum_pool(name="psum_ht", bufs=3))
+        psum_h1 = ctx.enter_context(tc.psum_pool(name="psum_h1", bufs=3))
+        psum_ht = ctx.enter_context(tc.psum_pool(name="psum_ht", bufs=2))
         psum_o = ctx.enter_context(tc.psum_pool(name="psum_o", bufs=2))
 
-        ident = const.tile([P, P], F32)
-        make_identity(nc, ident[:])
-        neg_half = const.tile([P, 1], F32)
-        nc.vector.memset(neg_half[:], -0.5)
+        experts = {}
+        tiles = {}
 
-        w1_planes = const.tile([P, EXPERTS // PLANES_PER_TILE, H], U8, align_bytes=64)
-        w2_planes = const.tile([P, EXPERTS * H_PASSES // PLANES_PER_TILE, D], U8, align_bytes=64)
-        nc.vector.memset(w1_planes[:].rearrange("p b n -> p (b n)").bitcast(I32), 0)
-        nc.vector.memset(w2_planes[:].rearrange("p b n -> p (b n)").bitcast(I32), 0)
+        def expert_of(j):
+            return j // TILES_PER_EXPERT
+
+        def dram_rows(tensor, j):
+            e, i = divmod(j, TILES_PER_EXPERT)
+            return tensor[B_TILE * i : B_TILE * (i + 1), e].rearrange("b t d -> t b d")
 
         def load_planes(planes, scales, block):
             first = PLANES_PER_TILE * block
@@ -67,27 +66,6 @@ def tile_hdmodel_pb_t_e_kernel(
                     ].bitcast(I32),
                 )
 
-        def rows_to_columns(x_rows):
-            words = x_rows[:].bitcast(F32)
-            x_cols = psum_x.tile([P, 2, P], F32)
-            for u in range(2):
-                nc.tensor.transpose(x_cols[:, u, :], words[:, u : D // 2 : 2], ident[:])
-            return x_cols
-
-        te_rows = const.tile([P, D], BF16)
-        nc.sync.dma_start(
-            out=te_rows[:], in_=task_emb.unsqueeze(1).to_broadcast([TASKS, B_TILE, D])
-        )
-        te_psum = rows_to_columns(te_rows)
-        te_cols = const.tile([P, P, PACK], BF16)
-        nc.vector.tensor_copy(
-            out=te_cols[:].rearrange("p r t -> p (r t)").bitcast(F32).rearrange("p (r u) -> p r u", u=2),
-            in_=te_psum[:].rearrange("p u r -> p r u"),
-        )
-
-        experts = {}
-        tiles = {}
-
         def load_expert(e):
             if e % PLANES_PER_TILE == 0:
                 load_planes(w1_planes, W1_scales, e // PLANES_PER_TILE)
@@ -98,6 +76,8 @@ def tile_hdmodel_pb_t_e_kernel(
             )
             b1_rows = expert_pool.tile([P, H], BF16)
             nc.sync.dma_start(out=b1_rows[:], in_=b1[e].partition_broadcast(P))
+            b2_rows = expert_pool.tile([P, D], BF16)
+            nc.sync.dma_start(out=b2_rows[:], in_=b2[e].partition_broadcast(P))
             if (e * H_PASSES) % PLANES_PER_TILE == 0:
                 load_planes(w2_planes, W2_scales, e * H_PASSES // PLANES_PER_TILE)
             w2_words = expert_pool.tile([P, H_PASSES, PACK * D], U8, align_bytes=64)
@@ -106,101 +86,110 @@ def tile_hdmodel_pb_t_e_kernel(
                     out=w2_words[:, c, :].bitcast(I32),
                     in_=W2_words[e * H_PASSES + c].rearrange("p n t -> p (n t)").bitcast(I32),
                 )
-            b2_rows = expert_pool.tile([P, D], BF16)
-            nc.sync.dma_start(out=b2_rows[:], in_=b2[e].partition_broadcast(P))
             gain_rows = expert_pool.tile([P, D], BF16)
             nc.sync.dma_start(out=gain_rows[:], in_=ln_g[e].partition_broadcast(P))
             bias_rows = expert_pool.tile([P, D], BF16)
             nc.sync.dma_start(out=bias_rows[:], in_=ln_b[e].partition_broadcast(P))
-            te_b2 = expert_pool.tile([P, D], F32)
-            nc.gpsimd.tensor_tensor(out=te_b2[:], in0=te_rows[:], in1=b2_rows[:], op=ALU.add)
             experts[e] = dict(
-                w1_words=w1_words, b1_rows=b1_rows, w2_words=w2_words,
-                gain_rows=gain_rows, bias_rows=bias_rows, te_b2=te_b2,
+                w1_words=w1_words, b1_rows=b1_rows, b2_rows=b2_rows, w2_words=w2_words,
+                gain_rows=gain_rows, bias_rows=bias_rows,
             )
-
-        def dram_rows(tensor, j):
-            e, i = divmod(j, TILES_PER_EXPERT)
-            return tensor[B_TILE * i : B_TILE * (i + 1), e].rearrange("b t d -> t b d")
 
         def load_rows(j):
             x_rows = rows_pool.tile([P, D], BF16)
             nc.sync.dma_start(out=x_rows[:], in_=dram_rows(xs_mix, j))
             tiles[j] = dict(x_rows=x_rows)
 
-        def stage_1_quantise_rows(j):
-            x_cols = rows_to_columns(tiles[j]["x_rows"])
-            x_grouped = xq_pool.tile([P, P, PACK], BF16, align_bytes=64)
+        def transpose_rows(x_rows):
+            words = x_rows[:].bitcast(F32)
+            x_cols = psum_x.tile([P, 2, P], F32)
+            for u in range(2):
+                nc.tensor.transpose(x_cols[:, u, :], words[:, u : D // 2 : 2], ident[:])
+            return x_cols
+
+        def add_task_embedding(j):
+            x_grouped = work.tile([P, P, PACK], BF16, align_bytes=64)
             nc.vector.tensor_tensor(
                 out=x_grouped[:].rearrange("p r (u e) -> p r u e", e=2),
-                in0=x_cols[:].bitcast(BF16).rearrange("p u (r e) -> p r u e", e=2),
+                in0=tiles[j]["x_cols"][:].bitcast(BF16).rearrange("p u (r e) -> p r u e", e=2),
                 in1=te_cols[:].rearrange("p r (u e) -> p r u e", e=2),
                 op=ALU.add,
             )
-            x_codes = xq_pool.tile([P, P], U32, align_bytes=64)
-            x_scales = xq_pool.tile([P, P], U8, align_bytes=64)
+            tiles[j]["x_grouped"] = x_grouped
+
+        def quantise_rows(j):
+            x_codes = work.tile([P, P], U32, align_bytes=64)
+            x_scales = work.tile([P, P], U8, align_bytes=64)
             nc.vector.quantize_mx(
                 out=x_codes[:].bitcast(FP8X4),
                 scales=x_scales[:],
-                in_=x_grouped[:].rearrange("p r t -> p (r t)"),
+                in_=tiles[j]["x_grouped"][:].rearrange("p r t -> p (r t)"),
             )
             tiles[j]["x_codes"] = x_codes
             tiles[j]["x_scales"] = x_scales
 
-        def stage_2_first_matmul(j):
-            e = j // TILES_PER_EXPERT
+        def first_matmul(j):
+            e = expert_of(j)
             block, plane = divmod(e, PLANES_PER_TILE)
-            pre_act = []
+            tiles[j]["h_psum"] = []
             for c in range(H_PASSES):
-                cols = slice(K_PASS * c, K_PASS * (c + 1))
                 h_psum = psum_h1.tile([P, K_PASS], F32)
                 nc.tensor.matmul_mx(
                     out=h_psum[:],
                     lhsT=tiles[j]["x_codes"][:].bitcast(FP8X4),
                     lhsT_scale=tiles[j]["x_scales"][:],
                     rhs=experts[e]["w1_words"][:, PACK * K_PASS * c : PACK * K_PASS * (c + 1)].bitcast(FP8X4),
-                    rhs_scale=w1_planes[4 * plane : P, block, cols],
+                    rhs_scale=w1_planes[4 * plane : P, block, K_PASS * c : K_PASS * (c + 1)],
                     start=True,
                     stop=True,
                 )
-                h_sorted = hb_pool.tile([P, PACK, P], F32)
+                tiles[j]["h_psum"].append(h_psum)
+
+        def add_first_bias(j):
+            tiles[j]["h_sorted"] = []
+            for c in range(H_PASSES):
+                h_sorted = sorted_pool.tile([P, PACK, P], F32)
                 nc.vector.tensor_tensor(
                     out=h_sorted[:],
-                    in0=h_psum[:].rearrange("r (p t) -> r t p", t=PACK),
-                    in1=experts[e]["b1_rows"][:, cols].rearrange("r (p t) -> r t p", t=PACK),
+                    in0=tiles[j]["h_psum"][c][:].rearrange("r (p t) -> r t p", t=PACK),
+                    in1=experts[expert_of(j)]["b1_rows"][:, K_PASS * c : K_PASS * (c + 1)].rearrange(
+                        "r (p t) -> r t p", t=PACK
+                    ),
                     op=ALU.add,
                 )
-                pre_act.append(h_sorted)
-            resid = resid_pool.tile([P, D], F32)
-            nc.gpsimd.tensor_tensor(
-                out=resid[:], in0=tiles[j]["x_rows"][:], in1=experts[e]["te_b2"][:], op=ALU.add
-            )
-            tiles[j]["pre_act"] = pre_act
-            tiles[j]["resid"] = resid
+                tiles[j]["h_sorted"].append(h_sorted)
 
-        def stage_3_quantise_hidden(j):
-            h_grouped = hq_pool.tile([P, H_PASSES, P, PACK], BF16, align_bytes=64)
+        def transpose_hidden(j):
+            tiles[j]["h_cols"] = []
             for c in range(H_PASSES):
                 h_cols = psum_ht.tile([P, PACK, P], F32)
                 for t in range(PACK):
-                    nc.tensor.transpose(h_cols[:, t, :], tiles[j]["pre_act"][c][:, t, :], ident[:])
+                    nc.tensor.transpose(h_cols[:, t, :], tiles[j]["h_sorted"][c][:, t, :], ident[:])
+                tiles[j]["h_cols"].append(h_cols)
+
+        def silu(j):
+            h_grouped = work.tile([P, H_PASSES, P, PACK], BF16, align_bytes=64)
+            for c in range(H_PASSES):
                 nc.scalar.activation(
                     out=h_grouped[:, c, :, :],
-                    in_=h_cols[:].rearrange("p t r -> p r t"),
+                    in_=tiles[j]["h_cols"][c][:].rearrange("p t r -> p r t"),
                     func=ACT.Silu,
                 )
-            h_codes = hq_pool.tile([P, H_PASSES * P], U32, align_bytes=64)
-            h_scales = hq_pool.tile([P, H_PASSES * P], U8, align_bytes=64)
+            tiles[j]["h_grouped"] = h_grouped
+
+        def quantise_hidden(j):
+            h_codes = work.tile([P, H_PASSES * P], U32, align_bytes=64)
+            h_scales = work.tile([P, H_PASSES * P], U8, align_bytes=64)
             nc.vector.quantize_mx(
                 out=h_codes[:].bitcast(FP8X4),
                 scales=h_scales[:],
-                in_=h_grouped[:].rearrange("p c r t -> p (c r t)"),
+                in_=tiles[j]["h_grouped"][:].rearrange("p c r t -> p (c r t)"),
             )
             tiles[j]["h_codes"] = h_codes
             tiles[j]["h_scales"] = h_scales
 
-        def stage_4_second_matmul(j):
-            e = j // TILES_PER_EXPERT
+        def second_matmul(j):
+            e = expert_of(j)
             o_psum = psum_o.tile([P, D], F32)
             for c in range(H_PASSES):
                 block, plane = divmod(e * H_PASSES + c, PLANES_PER_TILE)
@@ -213,62 +202,132 @@ def tile_hdmodel_pb_t_e_kernel(
                     start=(c == 0),
                     stop=(c == H_PASSES - 1),
                 )
-            r = ln_pool.tile([P, D], F32)
+            tiles[j]["o_psum"] = o_psum
+
+        def expert_constant(e):
+            te_b2 = expert_pool.tile([P, D], F32)
+            nc.gpsimd.tensor_tensor(
+                out=te_b2[:], in0=te_rows[:], in1=experts[e]["b2_rows"][:], op=ALU.add
+            )
+            experts[e]["te_b2"] = te_b2
+
+        def residual_input(j):
+            resid = work.tile([P, D], F32)
+            nc.gpsimd.tensor_tensor(
+                out=resid[:], in0=tiles[j]["x_rows"][:], in1=experts[expert_of(j)]["te_b2"][:], op=ALU.add
+            )
+            tiles[j]["resid"] = resid
+
+        def add_residual(j):
+            r = work.tile([P, D], F32)
             r_sum = stat_pool.tile([P, 1], F32)
             nc.vector.scalar_tensor_tensor(
-                out=r[:], in0=o_psum[:], scalar=1.0, in1=tiles[j]["resid"][:],
+                out=r[:], in0=tiles[j]["o_psum"][:], scalar=1.0, in1=tiles[j]["resid"][:],
                 op0=ALU.mult, op1=ALU.add, accum_out=r_sum[:],
             )
+            tiles[j]["r"] = r
+            tiles[j]["r_sum"] = r_sum
+
+        def row_statistics(j):
             neg_mean = stat_pool.tile([P, 1], F32)
-            nc.gpsimd.tensor_scalar(
-                out=neg_mean[:], in0=r_sum[:], scalar1=-1.0 / D, scalar2=0.0, op0=ALU.mult, op1=ALU.add
-            )
-            squares = ln_pool.tile([P, D], BF16)
+            nc.scalar.activation(out=neg_mean[:], in_=tiles[j]["r_sum"][:], func=ACT.Copy, scale=-1.0 / D)
+            squares = work.tile([P, D], BF16)
             dev_sum = stat_pool.tile([P, 1], F32)
             nc.scalar.activation(
-                out=squares[:], in_=r[:], func=ACT.Square, bias=neg_mean[:, 0:1], scale=1.0,
+                out=squares[:], in_=tiles[j]["r"][:], func=ACT.Square, bias=neg_mean[:, 0:1], scale=1.0,
                 accum_out=dev_sum[:],
             )
-            tiles[j]["r"] = r
-            tiles[j]["neg_mean"] = neg_mean
-            tiles[j]["dev_sum"] = dev_sum
-
-        def stage_5_layer_norm(j):
-            e = j // TILES_PER_EXPERT
             var_eps = stat_pool.tile([P, 1], F32)
-            nc.gpsimd.tensor_scalar(
-                out=var_eps[:], in0=tiles[j]["dev_sum"][:], scalar1=1.0 / D, scalar2=LN_EPS,
-                op0=ALU.mult, op1=ALU.add,
-            )
+            nc.scalar.activation(out=var_eps[:], in_=dev_sum[:], func=ACT.Copy, scale=1.0 / D, bias=LN_EPS)
+            tiles[j]["neg_mean"] = neg_mean
+            tiles[j]["var_eps"] = var_eps
+
+        def inverse_std(j):
             rstd = stat_pool.tile([P, 1], F32)
-            nc.gpsimd.tensor_tensor(out=rstd[:], in0=var_eps[:], in1=neg_half[:], op=ALU.pow)
-            gained = ln_pool.tile([P, D], F32)
+            nc.gpsimd.tensor_tensor(out=rstd[:], in0=tiles[j]["var_eps"][:], in1=neg_half[:], op=ALU.pow)
+            tiles[j]["rstd"] = rstd
+
+        def centre_and_gain(j):
+            gained = work.tile([P, D], F32)
             nc.vector.scalar_tensor_tensor(
                 out=gained[:], in0=tiles[j]["r"][:], scalar=tiles[j]["neg_mean"][:, 0:1],
-                in1=experts[e]["gain_rows"][:], op0=ALU.add, op1=ALU.mult,
+                in1=experts[expert_of(j)]["gain_rows"][:], op0=ALU.add, op1=ALU.mult,
             )
-            scaled = ln_pool.tile([P, D], F32)
-            nc.scalar.activation(out=scaled[:], in_=gained[:], func=ACT.Copy, scale=rstd[:, 0:1])
-            y = ln_pool.tile([P, D], F32)
-            nc.gpsimd.tensor_tensor(out=y[:], in0=scaled[:], in1=experts[e]["bias_rows"][:], op=ALU.add)
+            tiles[j]["gained"] = gained
+
+        def scale_by_inverse_std(j):
+            scaled = work.tile([P, D], F32)
+            nc.scalar.activation(
+                out=scaled[:], in_=tiles[j]["gained"][:], func=ACT.Copy, scale=tiles[j]["rstd"][:, 0:1]
+            )
+            tiles[j]["scaled"] = scaled
+
+        def add_bias_and_store(j):
+            y = work.tile([P, D], F32)
+            nc.gpsimd.tensor_tensor(
+                out=y[:], in0=tiles[j]["scaled"][:], in1=experts[expert_of(j)]["bias_rows"][:], op=ALU.add
+            )
             nc.sync.dma_start(out=dram_rows(out, j), in_=y[:])
 
+        w1_planes = const.tile([P, EXPERTS // PLANES_PER_TILE, H], U8, align_bytes=64)
+        w2_planes = const.tile([P, EXPERTS * H_PASSES // PLANES_PER_TILE, D], U8, align_bytes=64)
+        nc.vector.memset(w1_planes[:].rearrange("p b n -> p (b n)").bitcast(I32), 0)
+        nc.vector.memset(w2_planes[:].rearrange("p b n -> p (b n)").bitcast(I32), 0)
+        neg_half = const.tile([P, 1], F32)
+        nc.vector.memset(neg_half[:], -0.5)
+        ident = const.tile([P, P], F32)
+        make_identity(nc, ident[:])
+
+        te_rows = const.tile([P, D], BF16)
+        nc.sync.dma_start(
+            out=te_rows[:], in_=task_emb.unsqueeze(1).to_broadcast([TASKS, B_TILE, D])
+        )
         load_rows(0)
         load_expert(0)
-        for j in range(1, ROWS_AHEAD):
+        for j in range(1, ROWS_AHEAD - 2):
             load_rows(j)
-        for step in range(N_TILES + 4):
-            if step % TILES_PER_EXPERT == 0 and step // TILES_PER_EXPERT + 1 < EXPERTS:
-                load_expert(step // TILES_PER_EXPERT + 1)
-            if step + ROWS_AHEAD < N_TILES:
-                load_rows(step + ROWS_AHEAD)
-            if step < N_TILES:
-                stage_1_quantise_rows(step)
-            if 0 <= step - 2 < N_TILES:
-                stage_3_quantise_hidden(step - 2)
-            if 0 <= step - 1 < N_TILES:
-                stage_2_first_matmul(step - 1)
-            if 0 <= step - 3 < N_TILES:
-                stage_4_second_matmul(step - 3)
-            if 0 <= step - 4 < N_TILES:
-                stage_5_layer_norm(step - 4)
+        te_psum = transpose_rows(te_rows)
+        te_cols = const.tile([P, P, PACK], BF16)
+        nc.vector.tensor_copy(
+            out=te_cols[:].rearrange("p r t -> p (r t)").bitcast(F32).rearrange("p (r u) -> p r u", u=2),
+            in_=te_psum[:].rearrange("p u r -> p r u"),
+        )
+        expert_constant(0)
+
+        def live(j):
+            return 0 <= j < N_TILES
+
+        for j in range(-2, N_TILES + 2):
+            if (j + EXPERT_AHEAD) % TILES_PER_EXPERT == 0 and 1 <= (j + EXPERT_AHEAD) // TILES_PER_EXPERT < EXPERTS:
+                load_expert((j + EXPERT_AHEAD) // TILES_PER_EXPERT)
+            if ROWS_AHEAD - 2 <= j + ROWS_AHEAD < N_TILES:
+                load_rows(j + ROWS_AHEAD)
+            if live(j - 2):
+                inverse_std(j - 2)
+                scale_by_inverse_std(j - 2)
+            if live(j + 2):
+                tiles[j + 2]["x_cols"] = transpose_rows(tiles[j + 2]["x_rows"])
+            if live(j):
+                add_first_bias(j)
+                transpose_hidden(j)
+                residual_input(j)
+            if live(j - 2):
+                add_bias_and_store(j - 2)
+            if live(j + 1) and (j + 1) % TILES_PER_EXPERT == 0 and j + 1 > 0:
+                expert_constant(expert_of(j + 1))
+            if live(j + 2):
+                add_task_embedding(j + 2)
+            if live(j):
+                silu(j)
+            if live(j + 1):
+                first_matmul(j + 1)
+            if live(j - 1):
+                add_residual(j - 1)
+                row_statistics(j - 1)
+            if live(j):
+                quantise_hidden(j)
+                second_matmul(j)
+            if live(j - 1):
+                centre_and_gain(j - 1)
+            if live(j + 2):
+                quantise_rows(j + 2)

@@ -25,6 +25,13 @@ H_PASSES = H // K_PASS
 PLANES_PER_TILE = 4
 ROWS_AHEAD = 5
 EXPERT_AHEAD = 6
+B1_COLS = slice(0, H)
+B2_COLS = slice(H, H + D)
+GAIN_COLS = slice(H + D, H + 2 * D)
+BIAS_COLS = slice(H + 2 * D, H + 3 * D)
+VECTOR_COLS = H + 3 * D
+SPREAD_COLS = 2 * K_PASS
+SPREAD_UNITS = -(-VECTOR_COLS // SPREAD_COLS)
 
 FLOPS = 2 * BATCH * EXPERTS * TASKS * (D * H + H * D)
 
@@ -42,7 +49,8 @@ def tile_hdmodel_pb_t_e_kernel(
         sorted_pool = ctx.enter_context(tc.tile_pool(name="sorted", bufs=2 * H_PASSES))
         stat_pool = ctx.enter_context(tc.tile_pool(name="stat", bufs=4))
         psum_x = ctx.enter_context(tc.psum_pool(name="psum_x", bufs=1))
-        psum_h1 = ctx.enter_context(tc.psum_pool(name="psum_h1", bufs=3))
+        psum_spread = ctx.enter_context(tc.psum_pool(name="psum_spread", bufs=1))
+        psum_h1 = ctx.enter_context(tc.psum_pool(name="psum_h1", bufs=2))
         psum_ht = ctx.enter_context(tc.psum_pool(name="psum_ht", bufs=2))
         psum_o = ctx.enter_context(tc.psum_pool(name="psum_o", bufs=2))
 
@@ -74,10 +82,6 @@ def tile_hdmodel_pb_t_e_kernel(
                 out=w1_words[:].bitcast(I32),
                 in_=W1_words[e].rearrange("p n t -> p (n t)").bitcast(I32),
             )
-            b1_rows = expert_pool.tile([P, H], BF16)
-            nc.sync.dma_start(out=b1_rows[:], in_=b1[e].partition_broadcast(P))
-            b2_rows = expert_pool.tile([P, D], BF16)
-            nc.sync.dma_start(out=b2_rows[:], in_=b2[e].partition_broadcast(P))
             if (e * H_PASSES) % PLANES_PER_TILE == 0:
                 load_planes(w2_planes, W2_scales, e * H_PASSES // PLANES_PER_TILE)
             w2_words = expert_pool.tile([P, H_PASSES, PACK * D], U8, align_bytes=64)
@@ -86,19 +90,29 @@ def tile_hdmodel_pb_t_e_kernel(
                     out=w2_words[:, c, :].bitcast(I32),
                     in_=W2_words[e * H_PASSES + c].rearrange("p n t -> p (n t)").bitcast(I32),
                 )
-            gain_rows = expert_pool.tile([P, D], BF16)
-            nc.sync.dma_start(out=gain_rows[:], in_=ln_g[e].partition_broadcast(P))
-            bias_rows = expert_pool.tile([P, D], BF16)
-            nc.sync.dma_start(out=bias_rows[:], in_=ln_b[e].partition_broadcast(P))
-            experts[e] = dict(
-                w1_words=w1_words, b1_rows=b1_rows, b2_rows=b2_rows, w2_words=w2_words,
-                gain_rows=gain_rows, bias_rows=bias_rows,
-            )
+            experts[e] = dict(w1_words=w1_words, w2_words=w2_words)
 
         def load_rows(j):
             x_rows = rows_pool.tile([P, D], BF16)
             nc.sync.dma_start(out=x_rows[:], in_=dram_rows(xs_mix, j))
             tiles[j] = dict(x_rows=x_rows)
+
+        def spread_vectors(e, unit):
+            if unit == 0:
+                vec_rows = expert_pool.tile([P, VECTOR_COLS], BF16)
+                experts[e]["vec_rows"] = vec_rows
+            first = SPREAD_COLS * unit
+            width = min(SPREAD_COLS, VECTOR_COLS - first)
+            spread = psum_spread.tile([P, SPREAD_COLS], BF16)
+            for c in range(0, width, K_PASS):
+                nc.tensor.matmul(
+                    out=spread[:, c : c + K_PASS],
+                    lhsT=ident_bf16[:, e : e + 1].to_broadcast([P, P]),
+                    rhs=vectors[:, first + c : first + c + K_PASS],
+                    start=True,
+                    stop=True,
+                )
+            nc.scalar.copy(out=experts[e]["vec_rows"][:, first : first + width], in_=spread[:, 0:width])
 
         def transpose_rows(x_rows):
             words = x_rows[:].bitcast(F32)
@@ -152,7 +166,7 @@ def tile_hdmodel_pb_t_e_kernel(
                 nc.vector.tensor_tensor(
                     out=h_sorted[:],
                     in0=tiles[j]["h_psum"][c][:].rearrange("r (p t) -> r t p", t=PACK),
-                    in1=experts[expert_of(j)]["b1_rows"][:, K_PASS * c : K_PASS * (c + 1)].rearrange(
+                    in1=experts[expert_of(j)]["vec_rows"][:, B1_COLS][:, K_PASS * c : K_PASS * (c + 1)].rearrange(
                         "r (p t) -> r t p", t=PACK
                     ),
                     op=ALU.add,
@@ -207,7 +221,7 @@ def tile_hdmodel_pb_t_e_kernel(
         def expert_constant(e):
             te_b2 = expert_pool.tile([P, D], F32)
             nc.gpsimd.tensor_tensor(
-                out=te_b2[:], in0=te_rows[:], in1=experts[e]["b2_rows"][:], op=ALU.add
+                out=te_b2[:], in0=te_rows[:], in1=experts[e]["vec_rows"][:, B2_COLS], op=ALU.add
             )
             experts[e]["te_b2"] = te_b2
 
@@ -251,7 +265,7 @@ def tile_hdmodel_pb_t_e_kernel(
             gained = work.tile([P, D], F32)
             nc.vector.scalar_tensor_tensor(
                 out=gained[:], in0=tiles[j]["r"][:], scalar=tiles[j]["neg_mean"][:, 0:1],
-                in1=experts[expert_of(j)]["gain_rows"][:], op0=ALU.add, op1=ALU.mult,
+                in1=experts[expert_of(j)]["vec_rows"][:, GAIN_COLS], op0=ALU.add, op1=ALU.mult,
             )
             tiles[j]["gained"] = gained
 
@@ -265,7 +279,7 @@ def tile_hdmodel_pb_t_e_kernel(
         def add_bias_and_store(j):
             y = work.tile([P, D], F32)
             nc.gpsimd.tensor_tensor(
-                out=y[:], in0=tiles[j]["scaled"][:], in1=experts[expert_of(j)]["bias_rows"][:], op=ALU.add
+                out=y[:], in0=tiles[j]["scaled"][:], in1=experts[expert_of(j)]["vec_rows"][:, BIAS_COLS], op=ALU.add
             )
             nc.sync.dma_start(out=dram_rows(out, j), in_=y[:])
 
@@ -277,12 +291,21 @@ def tile_hdmodel_pb_t_e_kernel(
         nc.vector.memset(neg_half[:], -0.5)
         ident = const.tile([P, P], F32)
         make_identity(nc, ident[:])
+        ident_bf16 = const.tile([P, P], BF16)
+        make_identity(nc, ident_bf16[:])
+
+        vectors = const.tile([P, VECTOR_COLS], BF16)
+        nc.vector.memset(vectors[:], 0.0)
 
         te_rows = const.tile([P, D], BF16)
         nc.sync.dma_start(
             out=te_rows[:], in_=task_emb.unsqueeze(1).to_broadcast([TASKS, B_TILE, D])
         )
         load_rows(0)
+        nc.sync.dma_start(out=vectors[0:EXPERTS, B1_COLS], in_=b1)
+        nc.sync.dma_start(out=vectors[0:EXPERTS, B2_COLS], in_=b2)
+        nc.sync.dma_start(out=vectors[0:EXPERTS, GAIN_COLS], in_=ln_g)
+        nc.sync.dma_start(out=vectors[0:EXPERTS, BIAS_COLS], in_=ln_b)
         load_expert(0)
         for j in range(1, ROWS_AHEAD - 2):
             load_rows(j)
@@ -292,42 +315,49 @@ def tile_hdmodel_pb_t_e_kernel(
             out=te_cols[:].rearrange("p r t -> p (r t)").bitcast(F32).rearrange("p (r u) -> p r u", u=2),
             in_=te_psum[:].rearrange("p u r -> p r u"),
         )
+        for unit in range(SPREAD_UNITS):
+            spread_vectors(0, unit)
         expert_constant(0)
 
         def live(j):
             return 0 <= j < N_TILES
 
-        for j in range(-2, N_TILES + 2):
+        for j in range(-2, N_TILES + 3):
             if (j + EXPERT_AHEAD) % TILES_PER_EXPERT == 0 and 1 <= (j + EXPERT_AHEAD) // TILES_PER_EXPERT < EXPERTS:
                 load_expert((j + EXPERT_AHEAD) // TILES_PER_EXPERT)
             if ROWS_AHEAD - 2 <= j + ROWS_AHEAD < N_TILES:
                 load_rows(j + ROWS_AHEAD)
+            next_expert = expert_of(j) + 1
+            prepare = j % TILES_PER_EXPERT if 0 <= j and next_expert < EXPERTS else None
             if live(j - 2):
                 inverse_std(j - 2)
-                scale_by_inverse_std(j - 2)
+            if live(j - 3):
+                scale_by_inverse_std(j - 3)
             if live(j + 2):
                 tiles[j + 2]["x_cols"] = transpose_rows(tiles[j + 2]["x_rows"])
             if live(j):
                 add_first_bias(j)
                 transpose_hidden(j)
                 residual_input(j)
-            if live(j - 2):
-                add_bias_and_store(j - 2)
-            if live(j + 1) and (j + 1) % TILES_PER_EXPERT == 0 and j + 1 > 0:
-                expert_constant(expert_of(j + 1))
+            if live(j - 3):
+                add_bias_and_store(j - 3)
+            if prepare == TILES_PER_EXPERT - 1:
+                expert_constant(next_expert)
             if live(j + 2):
                 add_task_embedding(j + 2)
             if live(j):
                 silu(j)
             if live(j + 1):
                 first_matmul(j + 1)
+            if prepare is not None and prepare < SPREAD_UNITS:
+                spread_vectors(next_expert, prepare)
             if live(j - 1):
                 add_residual(j - 1)
                 row_statistics(j - 1)
             if live(j):
                 quantise_hidden(j)
                 second_matmul(j)
-            if live(j - 1):
-                centre_and_gain(j - 1)
+            if live(j - 2):
+                centre_and_gain(j - 2)
             if live(j + 2):
                 quantise_rows(j + 2)

@@ -19,19 +19,20 @@ BATCH, EXPERTS, TASKS, D, H = 32, 8, 16, 512, 1024
 LN_EPS = 1e-5
 
 B_TILE = P // TASKS
-TILES_PER_EXPERT = BATCH // B_TILE
-N_TILES = EXPERTS * TILES_PER_EXPERT
+PAIR = 2
+ROWS = PAIR * P
+PAIRS_PER_EXPERT = BATCH // (B_TILE * PAIR)
+N_PAIRS = EXPERTS * PAIRS_PER_EXPERT
 H_PASSES = H // K_PASS
 PLANES_PER_TILE = 4
-ROWS_AHEAD = 5
-EXPERT_AHEAD = 6
-B1_COLS = slice(0, H)
-B2_COLS = slice(H, H + D)
-GAIN_COLS = slice(H + D, H + 2 * D)
-BIAS_COLS = slice(H + 2 * D, H + 3 * D)
-VECTOR_COLS = H + 3 * D
-SPREAD_COLS = 2 * K_PASS
-SPREAD_UNITS = -(-VECTOR_COLS // SPREAD_COLS)
+ROWS_AHEAD = 4
+EXPERT_AHEAD = 4
+TE_ROW = 0
+B2_ROW = TE_ROW + TASKS
+GAIN_ROW = B2_ROW + EXPERTS
+BIAS_ROW = GAIN_ROW + EXPERTS
+B1_ROW = BIAS_ROW + EXPERTS
+B1_ROWS = EXPERTS * H_PASSES
 
 FLOPS = 2 * BATCH * EXPERTS * TASKS * (D * H + H * D)
 
@@ -46,23 +47,22 @@ def tile_hdmodel_pb_t_e_kernel(
         expert_pool = ctx.enter_context(tc.tile_pool(name="expert", bufs=3))
         rows_pool = ctx.enter_context(tc.tile_pool(name="rows", bufs=ROWS_AHEAD + 2))
         work = ctx.enter_context(tc.tile_pool(name="work", bufs=3))
-        sorted_pool = ctx.enter_context(tc.tile_pool(name="sorted", bufs=2 * H_PASSES))
         stat_pool = ctx.enter_context(tc.tile_pool(name="stat", bufs=4))
         psum_x = ctx.enter_context(tc.psum_pool(name="psum_x", bufs=1))
         psum_spread = ctx.enter_context(tc.psum_pool(name="psum_spread", bufs=1))
-        psum_h1 = ctx.enter_context(tc.psum_pool(name="psum_h1", bufs=2))
-        psum_ht = ctx.enter_context(tc.psum_pool(name="psum_ht", bufs=2))
+        psum_h = ctx.enter_context(tc.psum_pool(name="psum_h", bufs=4))
         psum_o = ctx.enter_context(tc.psum_pool(name="psum_o", bufs=2))
 
         experts = {}
         tiles = {}
 
         def expert_of(j):
-            return j // TILES_PER_EXPERT
+            return j // PAIRS_PER_EXPERT
 
-        def dram_rows(tensor, j):
-            e, i = divmod(j, TILES_PER_EXPERT)
-            return tensor[B_TILE * i : B_TILE * (i + 1), e].rearrange("b t d -> t b d")
+        def dram_rows(tensor, j, i):
+            e, pair = divmod(j, PAIRS_PER_EXPERT)
+            first = B_TILE * (PAIR * pair + i)
+            return tensor[first : first + B_TILE, e].rearrange("b t d -> t b d")
 
         def load_planes(planes, scales, block):
             first = PLANES_PER_TILE * block
@@ -76,7 +76,7 @@ def tile_hdmodel_pb_t_e_kernel(
 
         def load_expert(e):
             if e % PLANES_PER_TILE == 0:
-                load_planes(w1_planes, W1_scales, e // PLANES_PER_TILE)
+                load_planes(w1_planes_raw, W1_scales, e // PLANES_PER_TILE)
             w1_words = expert_pool.tile([P, PACK * H], U8, align_bytes=64)
             nc.sync.dma_start(
                 out=w1_words[:].bitcast(I32),
@@ -90,39 +90,58 @@ def tile_hdmodel_pb_t_e_kernel(
                     out=w2_words[:, c, :].bitcast(I32),
                     in_=W2_words[e * H_PASSES + c].rearrange("p n t -> p (n t)").bitcast(I32),
                 )
-            experts[e] = dict(w1_words=w1_words, w2_words=w2_words)
+            experts[e] = dict(w1_raw=w1_words, w2_words=w2_words)
 
         def load_rows(j):
-            x_rows = rows_pool.tile([P, D], BF16)
-            nc.sync.dma_start(out=x_rows[:], in_=dram_rows(xs_mix, j))
+            x_rows = rows_pool.tile([P, PAIR, D], BF16)
+            for i in range(PAIR):
+                nc.sync.dma_start(out=x_rows[:, i, :], in_=dram_rows(xs_mix, j, i))
             tiles[j] = dict(x_rows=x_rows)
 
-        def spread_vectors(e, unit):
-            if unit == 0:
-                vec_rows = expert_pool.tile([P, VECTOR_COLS], BF16)
-                experts[e]["vec_rows"] = vec_rows
-            first = SPREAD_COLS * unit
-            width = min(SPREAD_COLS, VECTOR_COLS - first)
-            spread = psum_spread.tile([P, SPREAD_COLS], BF16)
-            for c in range(0, width, K_PASS):
-                nc.tensor.matmul(
-                    out=spread[:, c : c + K_PASS],
-                    lhsT=ident_bf16[:, e : e + 1].to_broadcast([P, P]),
-                    rhs=vectors[:, first + c : first + c + K_PASS],
-                    start=True,
-                    stop=True,
-                )
-            nc.scalar.copy(out=experts[e]["vec_rows"][:, first : first + width], in_=spread[:, 0:width])
+        def one_row(row):
+            return ident_bf16[:, row : row + 1].to_broadcast([P, P])
 
-        def transpose_rows(x_rows):
-            words = x_rows[:].bitcast(F32)
-            x_cols = psum_x.tile([P, 2, P], F32)
+        def spread_gain_and_bias(e):
+            gain_bias = psum_spread.tile([P, 2, D], BF16)
+            for i, row in enumerate((GAIN_ROW, BIAS_ROW)):
+                nc.tensor.matmul(out=gain_bias[:, i, :], lhsT=one_row(row + e), rhs=vectors[:], start=True, stop=True)
+            experts[e]["gain"] = gain_bias[:, 0, :]
+            experts[e]["bias"] = gain_bias[:, 1, :]
+
+        def expert_constant(e):
+            te_b2_psum = psum_o.tile([P, D], F32, name="o_psum")
+            nc.tensor.matmul(out=te_b2_psum[:], lhsT=task_of_row[:], rhs=vectors[:], start=True, stop=False)
+            nc.tensor.matmul(out=te_b2_psum[:], lhsT=one_row(B2_ROW + e), rhs=vectors[:], start=False, stop=True)
+            te_b2 = expert_pool.tile([P, D], F32)
+            nc.scalar.copy(out=te_b2[:], in_=te_b2_psum[:])
+            experts[e]["te_b2"] = te_b2
+
+        def sort_columns(e):
+            w1_words = expert_pool.tile([P, H_PASSES, PACK, P], I32, align_bytes=64)
+            raw = experts[e]["w1_raw"][:].bitcast(I32).rearrange("p (c m t) -> p c t m", c=H_PASSES, t=PACK)
+            for c in range(H_PASSES):
+                nc.vector.tensor_copy(out=w1_words[:, c], in_=raw[:, c])
+            experts[e]["w1_words"] = w1_words
+
+        def sort_plane_columns(block):
+            nc.vector.tensor_copy(
+                out=w1_planes[:, block, :].rearrange("p (c t m) -> p c t m", c=H_PASSES, t=PACK),
+                in_=w1_planes_raw[:, block, :].rearrange("p (c m t) -> p c t m", c=H_PASSES, t=PACK),
+            )
+
+        def transpose_rows(x_cols, i, x_rows):
+            words = x_rows.bitcast(F32)
             for u in range(2):
-                nc.tensor.transpose(x_cols[:, u, :], words[:, u : D // 2 : 2], ident[:])
-            return x_cols
+                nc.tensor.transpose(x_cols[:, u, P * i : P * (i + 1)], words[:, u : D // 2 : 2], ident[:])
+
+        def transpose_pair(j):
+            x_cols = psum_x.tile([P, 2, ROWS], F32)
+            for i in range(PAIR):
+                transpose_rows(x_cols, i, tiles[j]["x_rows"][:, i, :])
+            tiles[j]["x_cols"] = x_cols
 
         def add_task_embedding(j):
-            x_grouped = work.tile([P, P, PACK], BF16, align_bytes=64)
+            x_grouped = work.tile([P, ROWS, PACK], BF16, align_bytes=64)
             nc.vector.tensor_tensor(
                 out=x_grouped[:].rearrange("p r (u e) -> p r u e", e=2),
                 in0=tiles[j]["x_cols"][:].bitcast(BF16).rearrange("p u (r e) -> p r u e", e=2),
@@ -132,8 +151,8 @@ def tile_hdmodel_pb_t_e_kernel(
             tiles[j]["x_grouped"] = x_grouped
 
         def quantise_rows(j):
-            x_codes = work.tile([P, P], U32, align_bytes=64)
-            x_scales = work.tile([P, P], U8, align_bytes=64)
+            x_codes = work.tile([P, ROWS], U32, align_bytes=64)
+            x_scales = work.tile([P, ROWS], U8, align_bytes=64)
             nc.vector.quantize_mx(
                 out=x_codes[:].bitcast(FP8X4),
                 scales=x_scales[:],
@@ -147,56 +166,52 @@ def tile_hdmodel_pb_t_e_kernel(
             block, plane = divmod(e, PLANES_PER_TILE)
             tiles[j]["h_psum"] = []
             for c in range(H_PASSES):
-                h_psum = psum_h1.tile([P, K_PASS], F32)
-                nc.tensor.matmul_mx(
-                    out=h_psum[:],
-                    lhsT=tiles[j]["x_codes"][:].bitcast(FP8X4),
-                    lhsT_scale=tiles[j]["x_scales"][:],
-                    rhs=experts[e]["w1_words"][:, PACK * K_PASS * c : PACK * K_PASS * (c + 1)].bitcast(FP8X4),
-                    rhs_scale=w1_planes[4 * plane : P, block, K_PASS * c : K_PASS * (c + 1)],
-                    start=True,
-                    stop=True,
-                )
-                tiles[j]["h_psum"].append(h_psum)
-
-        def add_first_bias(j):
-            tiles[j]["h_sorted"] = []
-            for c in range(H_PASSES):
-                h_sorted = sorted_pool.tile([P, PACK, P], F32)
-                nc.vector.tensor_tensor(
-                    out=h_sorted[:],
-                    in0=tiles[j]["h_psum"][c][:].rearrange("r (p t) -> r t p", t=PACK),
-                    in1=experts[expert_of(j)]["vec_rows"][:, B1_COLS][:, K_PASS * c : K_PASS * (c + 1)].rearrange(
-                        "r (p t) -> r t p", t=PACK
-                    ),
-                    op=ALU.add,
-                )
-                tiles[j]["h_sorted"].append(h_sorted)
-
-        def transpose_hidden(j):
-            tiles[j]["h_cols"] = []
-            for c in range(H_PASSES):
-                h_cols = psum_ht.tile([P, PACK, P], F32)
-                for t in range(PACK):
-                    nc.tensor.transpose(h_cols[:, t, :], tiles[j]["h_sorted"][c][:, t, :], ident[:])
-                tiles[j]["h_cols"].append(h_cols)
+                for half in range(2):
+                    h_psum = psum_h.tile([P, 2, ROWS], F32)
+                    for t in range(2):
+                        first = K_PASS * c + P * (2 * half + t)
+                        nc.tensor.matmul_mx(
+                            out=h_psum[:, t, :],
+                            lhsT=experts[e]["w1_words"][:, c, 2 * half + t, :].bitcast(FP8X4),
+                            lhsT_scale=w1_planes[4 * plane : P, block, first : first + P],
+                            rhs=tiles[j]["x_codes"][:].bitcast(FP8X4),
+                            rhs_scale=tiles[j]["x_scales"][:],
+                            start=True,
+                            stop=True,
+                        )
+                    tiles[j]["h_psum"].append(h_psum)
 
         def silu(j):
-            h_grouped = work.tile([P, H_PASSES, P, PACK], BF16, align_bytes=64)
+            h_planes = work.tile([P, H_PASSES, PACK, ROWS], BF16, align_bytes=64)
             for c in range(H_PASSES):
-                nc.scalar.activation(
-                    out=h_grouped[:, c, :, :],
-                    in_=tiles[j]["h_cols"][c][:].rearrange("p t r -> p r t"),
-                    func=ACT.Silu,
-                )
+                for t in range(PACK):
+                    nc.scalar.activation(
+                        out=h_planes[:, c, t, :],
+                        in_=tiles[j]["h_psum"][2 * c + t // 2][:, t % 2, :],
+                        func=ACT.Silu,
+                        bias=b1_cols[:, expert_of(j) * H_PASSES + c, t : t + 1],
+                    )
+            tiles[j]["h_planes"] = h_planes
+
+        def interleave_hidden(j):
+            h_grouped = work.tile([P, H_PASSES, ROWS, PACK], BF16, align_bytes=64)
+            nc.scalar.copy(
+                out=h_grouped[:, 0].rearrange("p (q i) t -> p q t i", i=4),
+                in_=tiles[j]["h_planes"][:, 0].rearrange("p t (q i) -> p q t i", i=4),
+            )
+            nc.gpsimd.tensor_scalar(
+                out=h_grouped[:, 1],
+                in0=tiles[j]["h_planes"][:, 1].rearrange("p t r -> p r t"),
+                scalar1=1.0, scalar2=0.0, op0=ALU.mult, op1=ALU.add,
+            )
             tiles[j]["h_grouped"] = h_grouped
 
         def quantise_hidden(j):
-            h_codes = work.tile([P, H_PASSES * P], U32, align_bytes=64)
-            h_scales = work.tile([P, H_PASSES * P], U8, align_bytes=64)
+            h_codes = work.tile([P, H_PASSES, ROWS], U32, align_bytes=64)
+            h_scales = work.tile([P, H_PASSES, ROWS], U8, align_bytes=64)
             nc.vector.quantize_mx(
-                out=h_codes[:].bitcast(FP8X4),
-                scales=h_scales[:],
+                out=h_codes[:].rearrange("p c r -> p (c r)").bitcast(FP8X4),
+                scales=h_scales[:].rearrange("p c r -> p (c r)"),
                 in_=tiles[j]["h_grouped"][:].rearrange("p c r t -> p (c r t)"),
             )
             tiles[j]["h_codes"] = h_codes
@@ -204,160 +219,176 @@ def tile_hdmodel_pb_t_e_kernel(
 
         def second_matmul(j):
             e = expert_of(j)
-            o_psum = psum_o.tile([P, D], F32)
-            for c in range(H_PASSES):
-                block, plane = divmod(e * H_PASSES + c, PLANES_PER_TILE)
-                nc.tensor.matmul_mx(
-                    out=o_psum[:],
-                    lhsT=tiles[j]["h_codes"][:, P * c : P * (c + 1)].bitcast(FP8X4),
-                    lhsT_scale=tiles[j]["h_scales"][:, P * c : P * (c + 1)],
-                    rhs=experts[e]["w2_words"][:, c, :].bitcast(FP8X4),
-                    rhs_scale=w2_planes[4 * plane : P, block, :],
-                    start=(c == 0),
-                    stop=(c == H_PASSES - 1),
-                )
-            tiles[j]["o_psum"] = o_psum
-
-        def expert_constant(e):
-            te_b2 = expert_pool.tile([P, D], F32)
-            nc.gpsimd.tensor_tensor(
-                out=te_b2[:], in0=te_rows[:], in1=experts[e]["vec_rows"][:, B2_COLS], op=ALU.add
-            )
-            experts[e]["te_b2"] = te_b2
+            tiles[j]["o_psum"] = []
+            for i in range(PAIR):
+                o_psum = psum_o.tile([P, D], F32)
+                for c in range(H_PASSES):
+                    block, plane = divmod(e * H_PASSES + c, PLANES_PER_TILE)
+                    nc.tensor.matmul_mx(
+                        out=o_psum[:],
+                        lhsT=tiles[j]["h_codes"][:, c, P * i : P * (i + 1)].bitcast(FP8X4),
+                        lhsT_scale=tiles[j]["h_scales"][:, c, P * i : P * (i + 1)],
+                        rhs=experts[e]["w2_words"][:, c, :].bitcast(FP8X4),
+                        rhs_scale=w2_planes[4 * plane : P, block, :],
+                        start=(c == 0),
+                        stop=(c == H_PASSES - 1),
+                    )
+                tiles[j]["o_psum"].append(o_psum)
 
         def residual_input(j):
-            resid = work.tile([P, D], F32)
+            resid = work.tile([P, PAIR, D], F32)
             nc.gpsimd.tensor_tensor(
-                out=resid[:], in0=tiles[j]["x_rows"][:], in1=experts[expert_of(j)]["te_b2"][:], op=ALU.add
+                out=resid[:],
+                in0=tiles[j]["x_rows"][:],
+                in1=experts[expert_of(j)]["te_b2"][:].unsqueeze(1).to_broadcast([P, PAIR, D]),
+                op=ALU.add,
             )
             tiles[j]["resid"] = resid
 
         def add_residual(j):
-            r = work.tile([P, D], F32)
-            r_sum = stat_pool.tile([P, 1], F32)
-            nc.vector.scalar_tensor_tensor(
-                out=r[:], in0=tiles[j]["o_psum"][:], scalar=1.0, in1=tiles[j]["resid"][:],
-                op0=ALU.mult, op1=ALU.add, accum_out=r_sum[:],
-            )
+            r = work.tile([P, PAIR, D], F32)
+            r_sum = stat_pool.tile([P, PAIR], F32)
+            for i in range(PAIR):
+                nc.vector.scalar_tensor_tensor(
+                    out=r[:, i, :], in0=tiles[j]["o_psum"][i][:], scalar=1.0, in1=tiles[j]["resid"][:, i, :],
+                    op0=ALU.mult, op1=ALU.add, accum_out=r_sum[:, i : i + 1],
+                )
             tiles[j]["r"] = r
             tiles[j]["r_sum"] = r_sum
 
         def row_statistics(j):
-            neg_mean = stat_pool.tile([P, 1], F32)
+            neg_mean = stat_pool.tile([P, PAIR], F32)
             nc.scalar.activation(out=neg_mean[:], in_=tiles[j]["r_sum"][:], func=ACT.Copy, scale=-1.0 / D)
             squares = work.tile([P, D], BF16)
-            dev_sum = stat_pool.tile([P, 1], F32)
-            nc.scalar.activation(
-                out=squares[:], in_=tiles[j]["r"][:], func=ACT.Square, bias=neg_mean[:, 0:1], scale=1.0,
-                accum_out=dev_sum[:],
-            )
-            var_eps = stat_pool.tile([P, 1], F32)
+            dev_sum = stat_pool.tile([P, PAIR], F32)
+            for i in range(PAIR):
+                nc.scalar.activation(
+                    out=squares[:], in_=tiles[j]["r"][:, i, :], func=ACT.Square, bias=neg_mean[:, i : i + 1],
+                    scale=1.0, accum_out=dev_sum[:, i : i + 1],
+                )
+            var_eps = stat_pool.tile([P, PAIR], F32)
             nc.scalar.activation(out=var_eps[:], in_=dev_sum[:], func=ACT.Copy, scale=1.0 / D, bias=LN_EPS)
             tiles[j]["neg_mean"] = neg_mean
             tiles[j]["var_eps"] = var_eps
 
         def inverse_std(j):
-            rstd = stat_pool.tile([P, 1], F32)
+            rstd = stat_pool.tile([P, PAIR], F32)
             nc.gpsimd.tensor_tensor(out=rstd[:], in0=tiles[j]["var_eps"][:], in1=neg_half[:], op=ALU.pow)
             tiles[j]["rstd"] = rstd
 
         def centre_and_gain(j):
-            gained = work.tile([P, D], F32)
-            nc.vector.scalar_tensor_tensor(
-                out=gained[:], in0=tiles[j]["r"][:], scalar=tiles[j]["neg_mean"][:, 0:1],
-                in1=experts[expert_of(j)]["vec_rows"][:, GAIN_COLS], op0=ALU.add, op1=ALU.mult,
-            )
+            gained = work.tile([P, PAIR, D], F32)
+            for i in range(PAIR):
+                nc.vector.scalar_tensor_tensor(
+                    out=gained[:, i, :], in0=tiles[j]["r"][:, i, :], scalar=tiles[j]["neg_mean"][:, i : i + 1],
+                    in1=experts[expert_of(j)]["gain"], op0=ALU.add, op1=ALU.mult,
+                )
             tiles[j]["gained"] = gained
 
-        def scale_by_inverse_std(j):
-            scaled = work.tile([P, D], F32)
-            nc.scalar.activation(
-                out=scaled[:], in_=tiles[j]["gained"][:], func=ACT.Copy, scale=tiles[j]["rstd"][:, 0:1]
-            )
-            tiles[j]["scaled"] = scaled
+        def scale_bias_and_store(j):
+            y = work.tile([P, PAIR, D], F32)
+            for i in range(PAIR):
+                nc.vector.scalar_tensor_tensor(
+                    out=y[:, i, :], in0=tiles[j]["gained"][:, i, :], scalar=tiles[j]["rstd"][:, i : i + 1],
+                    in1=experts[expert_of(j)]["bias"], op0=ALU.mult, op1=ALU.add,
+                )
+                nc.sync.dma_start(out=dram_rows(out, j, i), in_=y[:, i, :])
 
-        def add_bias_and_store(j):
-            y = work.tile([P, D], F32)
-            nc.gpsimd.tensor_tensor(
-                out=y[:], in0=tiles[j]["scaled"][:], in1=experts[expert_of(j)]["vec_rows"][:, BIAS_COLS], op=ALU.add
-            )
-            nc.sync.dma_start(out=dram_rows(out, j), in_=y[:])
-
+        w1_planes_raw = const.tile([P, EXPERTS // PLANES_PER_TILE, H], U8, align_bytes=64)
         w1_planes = const.tile([P, EXPERTS // PLANES_PER_TILE, H], U8, align_bytes=64)
         w2_planes = const.tile([P, EXPERTS * H_PASSES // PLANES_PER_TILE, D], U8, align_bytes=64)
-        nc.vector.memset(w1_planes[:].rearrange("p b n -> p (b n)").bitcast(I32), 0)
+        nc.vector.memset(w1_planes_raw[:].rearrange("p b n -> p (b n)").bitcast(I32), 0)
         nc.vector.memset(w2_planes[:].rearrange("p b n -> p (b n)").bitcast(I32), 0)
-        neg_half = const.tile([P, 1], F32)
+        neg_half = const.tile([P, PAIR], F32)
         nc.vector.memset(neg_half[:], -0.5)
         ident = const.tile([P, P], F32)
         make_identity(nc, ident[:])
         ident_bf16 = const.tile([P, P], BF16)
         make_identity(nc, ident_bf16[:])
 
-        vectors = const.tile([P, VECTOR_COLS], BF16)
+        vectors = const.tile([P, D], BF16)
         nc.vector.memset(vectors[:], 0.0)
 
-        te_rows = const.tile([P, D], BF16)
+        task_of_row = const.tile([P, P], BF16)
+        nc.vector.tensor_copy(
+            out=task_of_row[:].rearrange("p (k b) -> p k b", k=TASKS),
+            in_=ident_bf16[:, TE_ROW : TE_ROW + TASKS].unsqueeze(2).to_broadcast([P, TASKS, B_TILE]),
+        )
+
+        nc.sync.dma_start(out=vectors[TE_ROW : TE_ROW + TASKS, :], in_=task_emb)
+        for row, vector in ((B2_ROW, b2), (GAIN_ROW, ln_g), (BIAS_ROW, ln_b)):
+            nc.sync.dma_start(out=vectors[row : row + EXPERTS, :], in_=vector)
         nc.sync.dma_start(
-            out=te_rows[:], in_=task_emb.unsqueeze(1).to_broadcast([TASKS, B_TILE, D])
+            out=vectors[B1_ROW : B1_ROW + B1_ROWS, :], in_=b1.rearrange("e (c k) -> (e c) k", c=H_PASSES)
         )
         load_rows(0)
-        nc.sync.dma_start(out=vectors[0:EXPERTS, B1_COLS], in_=b1)
-        nc.sync.dma_start(out=vectors[0:EXPERTS, B2_COLS], in_=b2)
-        nc.sync.dma_start(out=vectors[0:EXPERTS, GAIN_COLS], in_=ln_g)
-        nc.sync.dma_start(out=vectors[0:EXPERTS, BIAS_COLS], in_=ln_b)
         load_expert(0)
         for j in range(1, ROWS_AHEAD - 2):
             load_rows(j)
-        te_psum = transpose_rows(te_rows)
-        te_cols = const.tile([P, P, PACK], BF16)
+        vector_psum = psum_x.tile([P, 2, ROWS], F32, name="x_cols")
+        transpose_rows(vector_psum, 0, vectors[:])
+        te_cols = const.tile([P, ROWS, PACK], BF16)
+        for i in range(PAIR):
+            nc.vector.tensor_copy(
+                out=te_cols[:, P * i : P * (i + 1), :].rearrange("p r t -> p (r t)").bitcast(F32).rearrange(
+                    "p (k b u) -> p k b u", k=TASKS, u=2
+                ),
+                in_=vector_psum[:, :, TE_ROW : TE_ROW + TASKS]
+                .rearrange("p u k -> p k u")
+                .unsqueeze(2)
+                .to_broadcast([P, TASKS, B_TILE, 2]),
+            )
+        b1_bf16 = const.tile([P, B1_ROWS, PACK], BF16)
         nc.vector.tensor_copy(
-            out=te_cols[:].rearrange("p r t -> p (r t)").bitcast(F32).rearrange("p (r u) -> p r u", u=2),
-            in_=te_psum[:].rearrange("p u r -> p r u"),
+            out=b1_bf16[:].rearrange("p r t -> p (r t)").bitcast(F32).rearrange("p (r u) -> p r u", u=2),
+            in_=vector_psum[:, :, B1_ROW : B1_ROW + B1_ROWS].rearrange("p u r -> p r u"),
         )
-        for unit in range(SPREAD_UNITS):
-            spread_vectors(0, unit)
+        b1_cols = const.tile([P, B1_ROWS, PACK], F32)
+        nc.vector.tensor_copy(out=b1_cols[:], in_=b1_bf16[:])
         expert_constant(0)
+        spread_gain_and_bias(0)
 
         def live(j):
-            return 0 <= j < N_TILES
+            return 0 <= j < N_PAIRS
 
-        for j in range(-2, N_TILES + 3):
-            if (j + EXPERT_AHEAD) % TILES_PER_EXPERT == 0 and 1 <= (j + EXPERT_AHEAD) // TILES_PER_EXPERT < EXPERTS:
-                load_expert((j + EXPERT_AHEAD) // TILES_PER_EXPERT)
-            if ROWS_AHEAD - 2 <= j + ROWS_AHEAD < N_TILES:
+        for j in range(-2, N_PAIRS + 2):
+            if (j + EXPERT_AHEAD) % PAIRS_PER_EXPERT == 0 and 1 <= expert_of(j + EXPERT_AHEAD) < EXPERTS:
+                load_expert(expert_of(j + EXPERT_AHEAD))
+            if ROWS_AHEAD - 2 <= j + ROWS_AHEAD < N_PAIRS:
                 load_rows(j + ROWS_AHEAD)
             next_expert = expert_of(j) + 1
-            prepare = j % TILES_PER_EXPERT if 0 <= j and next_expert < EXPERTS else None
+            prepare = j % PAIRS_PER_EXPERT if 0 <= j and next_expert < EXPERTS else None
             if live(j - 2):
                 inverse_std(j - 2)
-            if live(j - 3):
-                scale_by_inverse_std(j - 3)
+            if live(j - 1):
+                quantise_hidden(j - 1)
+                residual_input(j - 1)
             if live(j + 2):
-                tiles[j + 2]["x_cols"] = transpose_rows(tiles[j + 2]["x_rows"])
-            if live(j):
-                add_first_bias(j)
-                transpose_hidden(j)
-                residual_input(j)
-            if live(j - 3):
-                add_bias_and_store(j - 3)
-            if prepare == TILES_PER_EXPERT - 1:
-                expert_constant(next_expert)
-            if live(j + 2):
+                transpose_pair(j + 2)
                 add_task_embedding(j + 2)
-            if live(j):
-                silu(j)
+            if live(j - 1):
+                second_matmul(j - 1)
             if live(j + 1):
                 first_matmul(j + 1)
-            if prepare is not None and prepare < SPREAD_UNITS:
-                spread_vectors(next_expert, prepare)
-            if live(j - 1):
-                add_residual(j - 1)
-                row_statistics(j - 1)
             if live(j):
-                quantise_hidden(j)
-                second_matmul(j)
+                silu(j)
+                interleave_hidden(j)
             if live(j - 2):
                 centre_and_gain(j - 2)
             if live(j + 2):
                 quantise_rows(j + 2)
+            if live(j - 2):
+                scale_bias_and_store(j - 2)
+            if j == -2:
+                sort_plane_columns(0)
+                sort_columns(0)
+            if j % PAIRS_PER_EXPERT == PAIRS_PER_EXPERT - 1 and 1 <= expert_of(j) < EXPERTS:
+                spread_gain_and_bias(expert_of(j))
+            if live(j - 1):
+                add_residual(j - 1)
+                row_statistics(j - 1)
+            if prepare == 0:
+                expert_constant(next_expert)
+                if next_expert % PLANES_PER_TILE == 0:
+                    sort_plane_columns(next_expert // PLANES_PER_TILE)
+                sort_columns(next_expert)

@@ -363,9 +363,18 @@ def tile_hdmodel_pb_t_e_kernel(
             if live(j - 1):
                 quantise_hidden(j - 1)
                 residual_input(j - 1)
+            if live(j + 1):
+                quantise_rows(j + 1)
+            if prepare == 0:
+                if next_expert % PLANES_PER_TILE == 0:
+                    sort_plane_columns(next_expert // PLANES_PER_TILE)
+                sort_columns(next_expert)
             if live(j + 2):
                 transpose_pair(j + 2)
                 add_task_embedding(j + 2)
+            if j == -2:
+                sort_plane_columns(0)
+                sort_columns(0)
             if live(j - 1):
                 second_matmul(j - 1)
             if live(j + 1):
@@ -375,13 +384,8 @@ def tile_hdmodel_pb_t_e_kernel(
                 interleave_hidden(j)
             if live(j - 2):
                 centre_and_gain(j - 2)
-            if live(j + 2):
-                quantise_rows(j + 2)
             if live(j - 2):
                 scale_bias_and_store(j - 2)
-            if j == -2:
-                sort_plane_columns(0)
-                sort_columns(0)
             if j % PAIRS_PER_EXPERT == PAIRS_PER_EXPERT - 1 and 1 <= expert_of(j) < EXPERTS:
                 spread_gain_and_bias(expert_of(j))
             if live(j - 1):
@@ -389,6 +393,3 @@ def tile_hdmodel_pb_t_e_kernel(
                 row_statistics(j - 1)
             if prepare == 0:
                 expert_constant(next_expert)
-                if next_expert % PLANES_PER_TILE == 0:
-                    sort_plane_columns(next_expert // PLANES_PER_TILE)
-                sort_columns(next_expert)

@@ -25,8 +25,8 @@ PAIRS_PER_EXPERT = BATCH // (B_TILE * PAIR)
 N_PAIRS = EXPERTS * PAIRS_PER_EXPERT
 H_PASSES = H // K_PASS
 PLANES_PER_TILE = 4
-ROWS_AHEAD = 4
-EXPERT_AHEAD = 4
+ROWS_AHEAD = 5
+EXPERT_AHEAD = 5
 TE_ROW = 0
 B2_ROW = TE_ROW + TASKS
 GAIN_ROW = B2_ROW + EXPERTS
@@ -44,7 +44,7 @@ def tile_hdmodel_pb_t_e_kernel(
     with ExitStack() as ctx:
         ctx.enter_context(tc.manual_schedule())
         const = ctx.enter_context(tc.tile_pool(name="const", bufs=1))
-        expert_pool = ctx.enter_context(tc.tile_pool(name="expert", bufs=3))
+        expert_pool = ctx.enter_context(tc.tile_pool(name="expert", bufs=4))
         rows_pool = ctx.enter_context(tc.tile_pool(name="rows", bufs=ROWS_AHEAD + 2))
         work = ctx.enter_context(tc.tile_pool(name="work", bufs=3))
         stat_pool = ctx.enter_context(tc.tile_pool(name="stat", bufs=4))
@@ -117,11 +117,11 @@ def tile_hdmodel_pb_t_e_kernel(
             experts[e]["te_b2"] = te_b2
 
         def sort_columns(e):
-            w1_words = expert_pool.tile([P, H_PASSES, PACK, P], I32, align_bytes=64)
+            w1_sorted = expert_pool.tile([P, H_PASSES, PACK, P], I32, align_bytes=64)
             raw = experts[e]["w1_raw"][:].bitcast(I32).rearrange("p (c m t) -> p c t m", c=H_PASSES, t=PACK)
             for c in range(H_PASSES):
-                nc.vector.tensor_copy(out=w1_words[:, c], in_=raw[:, c])
-            experts[e]["w1_words"] = w1_words
+                nc.vector.tensor_copy(out=w1_sorted[:, c], in_=raw[:, c])
+            experts[e]["w1_words"] = w1_sorted
 
         def sort_plane_columns(block):
             nc.vector.tensor_copy(
@@ -164,8 +164,8 @@ def tile_hdmodel_pb_t_e_kernel(
         def first_matmul(j):
             e = expert_of(j)
             block, plane = divmod(e, PLANES_PER_TILE)
-            tiles[j]["h_psum"] = []
-            for c in range(H_PASSES):
+            tiles[j]["h_psum"] = {}
+            for c in reversed(range(H_PASSES)):
                 for half in range(2):
                     h_psum = psum_h.tile([P, 2, ROWS], F32)
                     for t in range(2):
@@ -179,15 +179,15 @@ def tile_hdmodel_pb_t_e_kernel(
                             start=True,
                             stop=True,
                         )
-                    tiles[j]["h_psum"].append(h_psum)
+                    tiles[j]["h_psum"][c, half] = h_psum
 
         def silu(j):
             h_planes = work.tile([P, H_PASSES, PACK, ROWS], BF16, align_bytes=64)
-            for c in range(H_PASSES):
+            for c in reversed(range(H_PASSES)):
                 for t in range(PACK):
                     nc.scalar.activation(
                         out=h_planes[:, c, t, :],
-                        in_=tiles[j]["h_psum"][2 * c + t // 2][:, t % 2, :],
+                        in_=tiles[j]["h_psum"][c, t // 2][:, t % 2, :],
                         func=ACT.Silu,
                         bias=b1_cols[:, expert_of(j) * H_PASSES + c, t : t + 1],
                     )
@@ -323,7 +323,7 @@ def tile_hdmodel_pb_t_e_kernel(
         )
         load_rows(0)
         load_expert(0)
-        for j in range(1, ROWS_AHEAD - 2):
+        for j in range(1, ROWS_AHEAD - 3):
             load_rows(j)
         vector_psum = psum_x.tile([P, 2, ROWS], F32, name="x_cols")
         transpose_rows(vector_psum, 0, vectors[:])
@@ -351,45 +351,46 @@ def tile_hdmodel_pb_t_e_kernel(
         def live(j):
             return 0 <= j < N_PAIRS
 
-        for j in range(-2, N_PAIRS + 2):
+        for j in range(-3, N_PAIRS + 2):
             if (j + EXPERT_AHEAD) % PAIRS_PER_EXPERT == 0 and 1 <= expert_of(j + EXPERT_AHEAD) < EXPERTS:
                 load_expert(expert_of(j + EXPERT_AHEAD))
-            if ROWS_AHEAD - 2 <= j + ROWS_AHEAD < N_PAIRS:
+            if j + ROWS_AHEAD < N_PAIRS:
                 load_rows(j + ROWS_AHEAD)
             next_expert = expert_of(j) + 1
-            prepare = j % PAIRS_PER_EXPERT if 0 <= j and next_expert < EXPERTS else None
-            if live(j - 2):
-                inverse_std(j - 2)
+            prepare = j >= 0 and j % PAIRS_PER_EXPERT == 0 and next_expert < EXPERTS
             if live(j - 1):
                 quantise_hidden(j - 1)
-                residual_input(j - 1)
             if live(j + 1):
                 quantise_rows(j + 1)
-            if prepare == 0:
+            if j == -1:
+                sort_plane_columns(0)
+                sort_columns(0)
+            if prepare:
                 if next_expert % PLANES_PER_TILE == 0:
                     sort_plane_columns(next_expert // PLANES_PER_TILE)
                 sort_columns(next_expert)
             if live(j + 2):
-                transpose_pair(j + 2)
                 add_task_embedding(j + 2)
-            if j == -2:
-                sort_plane_columns(0)
-                sort_columns(0)
             if live(j - 1):
                 second_matmul(j - 1)
             if live(j + 1):
                 first_matmul(j + 1)
+            if live(j + 3):
+                transpose_pair(j + 3)
             if live(j):
                 silu(j)
                 interleave_hidden(j)
+                residual_input(j)
             if live(j - 2):
                 centre_and_gain(j - 2)
+            if live(j - 1):
+                add_residual(j - 1)
             if live(j - 2):
                 scale_bias_and_store(j - 2)
             if j % PAIRS_PER_EXPERT == PAIRS_PER_EXPERT - 1 and 1 <= expert_of(j) < EXPERTS:
                 spread_gain_and_bias(expert_of(j))
             if live(j - 1):
-                add_residual(j - 1)
                 row_statistics(j - 1)
-            if prepare == 0:
+                inverse_std(j - 1)
+            if prepare:
                 expert_constant(next_expert)

@@ -25,8 +25,9 @@ PAIRS_PER_EXPERT = BATCH // (B_TILE * PAIR)
 N_PAIRS = EXPERTS * PAIRS_PER_EXPERT
 H_PASSES = H // K_PASS
 PLANES_PER_TILE = 4
-ROWS_AHEAD = 5
-EXPERT_AHEAD = 5
+ROWS_AHEAD = 6
+W1_AHEAD = 7
+W2_AHEAD = 4
 TE_ROW = 0
 B2_ROW = TE_ROW + TASKS
 GAIN_ROW = B2_ROW + EXPERTS
@@ -44,7 +45,7 @@ def tile_hdmodel_pb_t_e_kernel(
     with ExitStack() as ctx:
         ctx.enter_context(tc.manual_schedule())
         const = ctx.enter_context(tc.tile_pool(name="const", bufs=1))
-        expert_pool = ctx.enter_context(tc.tile_pool(name="expert", bufs=4))
+        expert_pool = ctx.enter_context(tc.tile_pool(name="expert", bufs=6))
         rows_pool = ctx.enter_context(tc.tile_pool(name="rows", bufs=ROWS_AHEAD + 2))
         work = ctx.enter_context(tc.tile_pool(name="work", bufs=3))
         stat_pool = ctx.enter_context(tc.tile_pool(name="stat", bufs=4))
@@ -74,14 +75,18 @@ def tile_hdmodel_pb_t_e_kernel(
                     ].bitcast(I32),
                 )
 
-        def load_expert(e):
+        def load_w1(e):
             if e % PLANES_PER_TILE == 0:
                 load_planes(w1_planes_raw, W1_scales, e // PLANES_PER_TILE)
-            w1_words = expert_pool.tile([P, PACK * H], U8, align_bytes=64)
-            nc.sync.dma_start(
-                out=w1_words[:].bitcast(I32),
-                in_=W1_words[e].rearrange("p n t -> p (n t)").bitcast(I32),
-            )
+            w1_words = expert_pool.tile([P, H_PASSES, PACK * K_PASS], U8, align_bytes=64)
+            for c in reversed(range(H_PASSES)):
+                nc.sync.dma_start(
+                    out=w1_words[:, c, :].bitcast(I32),
+                    in_=W1_words[e, :, K_PASS * c : K_PASS * (c + 1), :].rearrange("p n t -> p (n t)").bitcast(I32),
+                )
+            experts[e] = dict(w1_raw=w1_words)
+
+        def load_w2(e):
             if (e * H_PASSES) % PLANES_PER_TILE == 0:
                 load_planes(w2_planes, W2_scales, e * H_PASSES // PLANES_PER_TILE)
             w2_words = expert_pool.tile([P, H_PASSES, PACK * D], U8, align_bytes=64)
@@ -90,7 +95,7 @@ def tile_hdmodel_pb_t_e_kernel(
                     out=w2_words[:, c, :].bitcast(I32),
                     in_=W2_words[e * H_PASSES + c].rearrange("p n t -> p (n t)").bitcast(I32),
                 )
-            experts[e] = dict(w1_raw=w1_words, w2_words=w2_words)
+            experts[e]["w2_words"] = w2_words
 
         def load_rows(j):
             x_rows = rows_pool.tile([P, PAIR, D], BF16)
@@ -118,24 +123,27 @@ def tile_hdmodel_pb_t_e_kernel(
 
         def sort_columns(e):
             w1_sorted = expert_pool.tile([P, H_PASSES, PACK, P], I32, align_bytes=64)
-            raw = experts[e]["w1_raw"][:].bitcast(I32).rearrange("p (c m t) -> p c t m", c=H_PASSES, t=PACK)
-            for c in range(H_PASSES):
-                nc.vector.tensor_copy(out=w1_sorted[:, c], in_=raw[:, c])
+            for c in reversed(range(H_PASSES)):
+                if e % PLANES_PER_TILE == 0:
+                    block = e // PLANES_PER_TILE
+                    cols = slice(K_PASS * c, K_PASS * (c + 1))
+                    nc.vector.tensor_copy(
+                        out=w1_planes[:, block, cols].rearrange("p (t m) -> p t m", t=PACK),
+                        in_=w1_planes_raw[:, block, cols].rearrange("p (m t) -> p t m", t=PACK),
+                    )
+                nc.vector.tensor_copy(
+                    out=w1_sorted[:, c],
+                    in_=experts[e]["w1_raw"][:, c, :].bitcast(I32).rearrange("p (m t) -> p t m", t=PACK),
+                )
             experts[e]["w1_words"] = w1_sorted
-
-        def sort_plane_columns(block):
-            nc.vector.tensor_copy(
-                out=w1_planes[:, block, :].rearrange("p (c t m) -> p c t m", c=H_PASSES, t=PACK),
-                in_=w1_planes_raw[:, block, :].rearrange("p (c m t) -> p c t m", c=H_PASSES, t=PACK),
-            )
 
         def transpose_rows(x_cols, i, x_rows):
             words = x_rows.bitcast(F32)
             for u in range(2):
-                nc.tensor.transpose(x_cols[:, u, P * i : P * (i + 1)], words[:, u : D // 2 : 2], ident[:])
+                nc.tensor.transpose(x_cols[:, P * i : P * (i + 1), u], words[:, u : D // 2 : 2], ident[:])
 
         def transpose_pair(j):
-            x_cols = psum_x.tile([P, 2, ROWS], F32)
+            x_cols = psum_x.tile([P, ROWS, 2], F32)
             for i in range(PAIR):
                 transpose_rows(x_cols, i, tiles[j]["x_rows"][:, i, :])
             tiles[j]["x_cols"] = x_cols
@@ -143,9 +151,9 @@ def tile_hdmodel_pb_t_e_kernel(
         def add_task_embedding(j):
             x_grouped = work.tile([P, ROWS, PACK], BF16, align_bytes=64)
             nc.vector.tensor_tensor(
-                out=x_grouped[:].rearrange("p r (u e) -> p r u e", e=2),
-                in0=tiles[j]["x_cols"][:].bitcast(BF16).rearrange("p u (r e) -> p r u e", e=2),
-                in1=te_cols[:].rearrange("p r (u e) -> p r u e", e=2),
+                out=x_grouped[:].rearrange("p r t -> p (r t)"),
+                in0=tiles[j]["x_cols"][:].rearrange("p r u -> p (r u)").bitcast(BF16),
+                in1=te_cols[:].rearrange("p r t -> p (r t)"),
                 op=ALU.add,
             )
             tiles[j]["x_grouped"] = x_grouped
@@ -258,22 +266,28 @@ def tile_hdmodel_pb_t_e_kernel(
 
         def row_statistics(j):
             neg_mean = stat_pool.tile([P, PAIR], F32)
-            nc.scalar.activation(out=neg_mean[:], in_=tiles[j]["r_sum"][:], func=ACT.Copy, scale=-1.0 / D)
-            squares = work.tile([P, D], BF16)
             dev_sum = stat_pool.tile([P, PAIR], F32)
-            for i in range(PAIR):
-                nc.scalar.activation(
-                    out=squares[:], in_=tiles[j]["r"][:, i, :], func=ACT.Square, bias=neg_mean[:, i : i + 1],
-                    scale=1.0, accum_out=dev_sum[:, i : i + 1],
-                )
             var_eps = stat_pool.tile([P, PAIR], F32)
-            nc.scalar.activation(out=var_eps[:], in_=dev_sum[:], func=ACT.Copy, scale=1.0 / D, bias=LN_EPS)
-            tiles[j]["neg_mean"] = neg_mean
-            tiles[j]["var_eps"] = var_eps
-
-        def inverse_std(j):
             rstd = stat_pool.tile([P, PAIR], F32)
-            nc.gpsimd.tensor_tensor(out=rstd[:], in0=tiles[j]["var_eps"][:], in1=neg_half[:], op=ALU.pow)
+            squares = work.tile([P, D], BF16)
+            step = 1 if j == N_PAIRS - 1 else PAIR
+            for first in range(0, PAIR, step):
+                cols = slice(first, first + step)
+                nc.scalar.activation(
+                    out=neg_mean[:, cols], in_=tiles[j]["r_sum"][:, cols], func=ACT.Copy, scale=-1.0 / D
+                )
+                for i in range(first, first + step):
+                    nc.scalar.activation(
+                        out=squares[:], in_=tiles[j]["r"][:, i, :], func=ACT.Square, bias=neg_mean[:, i : i + 1],
+                        scale=1.0, accum_out=dev_sum[:, i : i + 1],
+                    )
+                nc.scalar.activation(
+                    out=var_eps[:, cols], in_=dev_sum[:, cols], func=ACT.Copy, scale=1.0 / D, bias=LN_EPS
+                )
+                nc.gpsimd.tensor_tensor(
+                    out=rstd[:, cols], in0=var_eps[:, cols], in1=neg_half[:, cols], op=ALU.pow
+                )
+            tiles[j]["neg_mean"] = neg_mean
             tiles[j]["rstd"] = rstd
 
         def centre_and_gain(j):
@@ -297,6 +311,8 @@ def tile_hdmodel_pb_t_e_kernel(
         w1_planes_raw = const.tile([P, EXPERTS // PLANES_PER_TILE, H], U8, align_bytes=64)
         w1_planes = const.tile([P, EXPERTS // PLANES_PER_TILE, H], U8, align_bytes=64)
         w2_planes = const.tile([P, EXPERTS * H_PASSES // PLANES_PER_TILE, D], U8, align_bytes=64)
+        vectors = const.tile([P, D], BF16)
+        nc.vector.memset(vectors[:], 0.0)
         nc.vector.memset(w1_planes_raw[:].rearrange("p b n -> p (b n)").bitcast(I32), 0)
         nc.vector.memset(w2_planes[:].rearrange("p b n -> p (b n)").bitcast(I32), 0)
         neg_half = const.tile([P, PAIR], F32)
@@ -306,9 +322,6 @@ def tile_hdmodel_pb_t_e_kernel(
         ident_bf16 = const.tile([P, P], BF16)
         make_identity(nc, ident_bf16[:])
 
-        vectors = const.tile([P, D], BF16)
-        nc.vector.memset(vectors[:], 0.0)
-
         task_of_row = const.tile([P, P], BF16)
         nc.vector.tensor_copy(
             out=task_of_row[:].rearrange("p (k b) -> p k b", k=TASKS),
@@ -316,16 +329,20 @@ def tile_hdmodel_pb_t_e_kernel(
         )
 
         nc.sync.dma_start(out=vectors[TE_ROW : TE_ROW + TASKS, :], in_=task_emb)
-        for row, vector in ((B2_ROW, b2), (GAIN_ROW, ln_g), (BIAS_ROW, ln_b)):
-            nc.sync.dma_start(out=vectors[row : row + EXPERTS, :], in_=vector)
         nc.sync.dma_start(
             out=vectors[B1_ROW : B1_ROW + B1_ROWS, :], in_=b1.rearrange("e (c k) -> (e c) k", c=H_PASSES)
         )
+        for row, vector in ((B2_ROW, b2), (GAIN_ROW, ln_g), (BIAS_ROW, ln_b)):
+            nc.scalar.dma_start(out=vectors[row : row + EXPERTS, :], in_=vector)
+        table_load = const.tile([P, 1], F32)
+        nc.scalar.activation(out=table_load[:], in_=neg_half[:, 0:1], func=ACT.Silu)
         load_rows(0)
-        load_expert(0)
-        for j in range(1, ROWS_AHEAD - 3):
-            load_rows(j)
-        vector_psum = psum_x.tile([P, 2, ROWS], F32, name="x_cols")
+        load_w1(0)
+        load_rows(1)
+        load_rows(2)
+        load_w1(1)
+        load_w2(0)
+        vector_psum = psum_h.tile([P, ROWS, 2], F32, name="h_psum")
         transpose_rows(vector_psum, 0, vectors[:])
         te_cols = const.tile([P, ROWS, PACK], BF16)
         for i in range(PAIR):
@@ -333,29 +350,25 @@ def tile_hdmodel_pb_t_e_kernel(
                 out=te_cols[:, P * i : P * (i + 1), :].rearrange("p r t -> p (r t)").bitcast(F32).rearrange(
                     "p (k b u) -> p k b u", k=TASKS, u=2
                 ),
-                in_=vector_psum[:, :, TE_ROW : TE_ROW + TASKS]
-                .rearrange("p u k -> p k u")
+                in_=vector_psum[:, TE_ROW : TE_ROW + TASKS, :]
                 .unsqueeze(2)
                 .to_broadcast([P, TASKS, B_TILE, 2]),
             )
         b1_bf16 = const.tile([P, B1_ROWS, PACK], BF16)
-        nc.vector.tensor_copy(
-            out=b1_bf16[:].rearrange("p r t -> p (r t)").bitcast(F32).rearrange("p (r u) -> p r u", u=2),
-            in_=vector_psum[:, :, B1_ROW : B1_ROW + B1_ROWS].rearrange("p u r -> p r u"),
-        )
         b1_cols = const.tile([P, B1_ROWS, PACK], F32)
-        nc.vector.tensor_copy(out=b1_cols[:], in_=b1_bf16[:])
-        expert_constant(0)
-        spread_gain_and_bias(0)
 
         def live(j):
             return 0 <= j < N_PAIRS
 
         for j in range(-3, N_PAIRS + 2):
-            if (j + EXPERT_AHEAD) % PAIRS_PER_EXPERT == 0 and 1 <= expert_of(j + EXPERT_AHEAD) < EXPERTS:
-                load_expert(expert_of(j + EXPERT_AHEAD))
-            if j + ROWS_AHEAD < N_PAIRS:
+            if 3 <= j + ROWS_AHEAD < N_PAIRS:
                 load_rows(j + ROWS_AHEAD)
+            e, pair = divmod(j + W1_AHEAD, PAIRS_PER_EXPERT)
+            if pair == 0 and 2 <= e < EXPERTS:
+                load_w1(e)
+            e, pair = divmod(j + W2_AHEAD, PAIRS_PER_EXPERT)
+            if pair == 0 and 1 <= e < EXPERTS:
+                load_w2(e)
             next_expert = expert_of(j) + 1
             prepare = j >= 0 and j % PAIRS_PER_EXPERT == 0 and next_expert < EXPERTS
             if live(j - 1):
@@ -363,20 +376,28 @@ def tile_hdmodel_pb_t_e_kernel(
             if live(j + 1):
                 quantise_rows(j + 1)
             if j == -1:
-                sort_plane_columns(0)
                 sort_columns(0)
-            if prepare:
-                if next_expert % PLANES_PER_TILE == 0:
-                    sort_plane_columns(next_expert // PLANES_PER_TILE)
-                sort_columns(next_expert)
             if live(j + 2):
                 add_task_embedding(j + 2)
+            if j == -2:
+                nc.vector.tensor_copy(
+                    out=b1_bf16[:].rearrange("p r t -> p (r t)").bitcast(F32).rearrange("p (r u) -> p r u", u=2),
+                    in_=vector_psum[:, B1_ROW : B1_ROW + B1_ROWS, :],
+                )
+                nc.vector.tensor_copy(out=b1_cols[:], in_=b1_bf16[:])
+            if j == -1:
+                sort_columns(1)
+            if j >= 0 and j % PAIRS_PER_EXPERT == 0 and next_expert + 1 < EXPERTS:
+                sort_columns(next_expert + 1)
             if live(j - 1):
                 second_matmul(j - 1)
             if live(j + 1):
                 first_matmul(j + 1)
             if live(j + 3):
                 transpose_pair(j + 3)
+            if j == -3:
+                expert_constant(0)
+                spread_gain_and_bias(0)
             if live(j):
                 silu(j)
                 interleave_hidden(j)
@@ -391,6 +412,5 @@ def tile_hdmodel_pb_t_e_kernel(
                 spread_gain_and_bias(expert_of(j))
             if live(j - 1):
                 row_statistics(j - 1)
-                inverse_std(j - 1)
             if prepare:
                 expert_constant(next_expert)

@@ -25,6 +25,7 @@ PAIRS_PER_EXPERT = BATCH // (B_TILE * PAIR)
 N_PAIRS = EXPERTS * PAIRS_PER_EXPERT
 H_PASSES = H // K_PASS
 PLANES_PER_TILE = 4
+GPSIMD_ROWS = 128
 ROWS_AHEAD = 6
 W1_AHEAD = 7
 W2_AHEAD = 4
@@ -203,15 +204,16 @@ def tile_hdmodel_pb_t_e_kernel(
 
         def interleave_hidden(j):
             h_grouped = work.tile([P, H_PASSES, ROWS, PACK], BF16, align_bytes=64)
-            nc.scalar.copy(
-                out=h_grouped[:, 0].rearrange("p (q i) t -> p q t i", i=4),
-                in_=tiles[j]["h_planes"][:, 0].rearrange("p t (q i) -> p q t i", i=4),
-            )
             nc.gpsimd.tensor_scalar(
-                out=h_grouped[:, 1],
-                in0=tiles[j]["h_planes"][:, 1].rearrange("p t r -> p r t"),
+                out=h_grouped[:, 1, 0:GPSIMD_ROWS],
+                in0=tiles[j]["h_planes"][:, 1, :, 0:GPSIMD_ROWS].rearrange("p t r -> p r t"),
                 scalar1=1.0, scalar2=0.0, op0=ALU.mult, op1=ALU.add,
             )
+            for c, first in ((1, GPSIMD_ROWS), (0, 0)):
+                nc.scalar.copy(
+                    out=h_grouped[:, c, first:ROWS].rearrange("p (q i) t -> p q t i", i=4),
+                    in_=tiles[j]["h_planes"][:, c, :, first:ROWS].rearrange("p t (q i) -> p q t i", i=4),
+                )
             tiles[j]["h_grouped"] = h_grouped
 
         def quantise_hidden(j):
@@ -328,15 +330,15 @@ def tile_hdmodel_pb_t_e_kernel(
             in_=ident_bf16[:, TE_ROW : TE_ROW + TASKS].unsqueeze(2).to_broadcast([P, TASKS, B_TILE]),
         )
 
-        nc.sync.dma_start(out=vectors[TE_ROW : TE_ROW + TASKS, :], in_=task_emb)
-        nc.sync.dma_start(
+        nc.scalar.dma_start(out=vectors[TE_ROW : TE_ROW + TASKS, :], in_=task_emb)
+        nc.scalar.dma_start(
             out=vectors[B1_ROW : B1_ROW + B1_ROWS, :], in_=b1.rearrange("e (c k) -> (e c) k", c=H_PASSES)
         )
+        load_rows(0)
         for row, vector in ((B2_ROW, b2), (GAIN_ROW, ln_g), (BIAS_ROW, ln_b)):
-            nc.scalar.dma_start(out=vectors[row : row + EXPERTS, :], in_=vector)
+            nc.sync.dma_start(out=vectors[row : row + EXPERTS, :], in_=vector)
         table_load = const.tile([P, 1], F32)
         nc.scalar.activation(out=table_load[:], in_=neg_half[:, 0:1], func=ACT.Silu)
-        load_rows(0)
         load_w1(0)
         load_rows(1)
         load_rows(2)
@@ -375,6 +377,8 @@ def tile_hdmodel_pb_t_e_kernel(
                 quantise_hidden(j - 1)
             if live(j + 1):
                 quantise_rows(j + 1)
+            if j == 0:
+                sort_columns(1)
             if j == -1:
                 sort_columns(0)
             if live(j + 2):
@@ -385,8 +389,6 @@ def tile_hdmodel_pb_t_e_kernel(
                     in_=vector_psum[:, B1_ROW : B1_ROW + B1_ROWS, :],
                 )
                 nc.vector.tensor_copy(out=b1_cols[:], in_=b1_bf16[:])
-            if j == -1:
-                sort_columns(1)
             if j >= 0 and j % PAIRS_PER_EXPERT == 0 and next_expert + 1 < EXPERTS:
                 sort_columns(next_expert + 1)
             if live(j - 1):

@@ -25,7 +25,7 @@ PAIRS_PER_EXPERT = BATCH // (B_TILE * PAIR)
 N_PAIRS = EXPERTS * PAIRS_PER_EXPERT
 H_PASSES = H // K_PASS
 PLANES_PER_TILE = 4
-GPSIMD_ROWS = 128
+GPSIMD_ROWS = 160
 ROWS_AHEAD = 6
 W1_AHEAD = 7
 W2_AHEAD = 4
@@ -33,7 +33,7 @@ TE_ROW = 0
 B2_ROW = TE_ROW + TASKS
 GAIN_ROW = B2_ROW + EXPERTS
 BIAS_ROW = GAIN_ROW + EXPERTS
-B1_ROW = BIAS_ROW + EXPERTS
+B1_ROW = TE_ROW + TASKS
 B1_ROWS = EXPERTS * H_PASSES
 
 FLOPS = 2 * BATCH * EXPERTS * TASKS * (D * H + H * D)
@@ -76,16 +76,21 @@ def tile_hdmodel_pb_t_e_kernel(
                     ].bitcast(I32),
                 )
 
+        def load_w1_chunk(e, c):
+            raw = expert_pool.tile([P, PACK * K_PASS], U8, name="w1_raw_%d" % c, align_bytes=64)
+            nc.sync.dma_start(
+                out=raw[:].bitcast(I32),
+                in_=W1_words[e, :, K_PASS * c : K_PASS * (c + 1), :].rearrange("p n t -> p (n t)").bitcast(I32),
+            )
+            w1_sorted = expert_pool.tile([P, PACK, P], I32, name="w1_sorted_%d" % c, align_bytes=64)
+            experts.setdefault(e, {})["w1_raw", c] = raw
+            experts[e]["w1_words", c] = w1_sorted
+
         def load_w1(e):
             if e % PLANES_PER_TILE == 0:
                 load_planes(w1_planes_raw, W1_scales, e // PLANES_PER_TILE)
-            w1_words = expert_pool.tile([P, H_PASSES, PACK * K_PASS], U8, align_bytes=64)
             for c in reversed(range(H_PASSES)):
-                nc.sync.dma_start(
-                    out=w1_words[:, c, :].bitcast(I32),
-                    in_=W1_words[e, :, K_PASS * c : K_PASS * (c + 1), :].rearrange("p n t -> p (n t)").bitcast(I32),
-                )
-            experts[e] = dict(w1_raw=w1_words)
+                load_w1_chunk(e, c)
 
         def load_w2(e):
             if (e * H_PASSES) % PLANES_PER_TILE == 0:
@@ -122,21 +127,18 @@ def tile_hdmodel_pb_t_e_kernel(
             nc.scalar.copy(out=te_b2[:], in_=te_b2_psum[:])
             experts[e]["te_b2"] = te_b2
 
-        def sort_columns(e):
-            w1_sorted = expert_pool.tile([P, H_PASSES, PACK, P], I32, align_bytes=64)
-            for c in reversed(range(H_PASSES)):
-                if e % PLANES_PER_TILE == 0:
-                    block = e // PLANES_PER_TILE
-                    cols = slice(K_PASS * c, K_PASS * (c + 1))
-                    nc.vector.tensor_copy(
-                        out=w1_planes[:, block, cols].rearrange("p (t m) -> p t m", t=PACK),
-                        in_=w1_planes_raw[:, block, cols].rearrange("p (m t) -> p t m", t=PACK),
-                    )
-                nc.vector.tensor_copy(
-                    out=w1_sorted[:, c],
-                    in_=experts[e]["w1_raw"][:, c, :].bitcast(I32).rearrange("p (m t) -> p t m", t=PACK),
-                )
-            experts[e]["w1_words"] = w1_sorted
+        def sort_plane_columns(block, c):
+            cols = slice(K_PASS * c, K_PASS * (c + 1))
+            nc.vector.tensor_copy(
+                out=w1_planes[:, block, cols].rearrange("p (t m) -> p m t", t=PACK),
+                in_=w1_planes_raw[:, block, cols].rearrange("p (m t) -> p m t", t=PACK),
+            )
+
+        def sort_columns(e, c):
+            nc.vector.tensor_copy(
+                out=experts[e]["w1_words", c][:].rearrange("p t m -> p m t"),
+                in_=experts[e]["w1_raw", c][:].bitcast(I32).rearrange("p (m t) -> p m t", t=PACK),
+            )
 
         def transpose_rows(x_cols, i, x_rows):
             words = x_rows.bitcast(F32)
@@ -181,7 +183,7 @@ def tile_hdmodel_pb_t_e_kernel(
                         first = K_PASS * c + P * (2 * half + t)
                         nc.tensor.matmul_mx(
                             out=h_psum[:, t, :],
-                            lhsT=experts[e]["w1_words"][:, c, 2 * half + t, :].bitcast(FP8X4),
+                            lhsT=experts[e]["w1_words", c][:, 2 * half + t, :].bitcast(FP8X4),
                             lhsT_scale=w1_planes[4 * plane : P, block, first : first + P],
                             rhs=tiles[j]["x_codes"][:].bitcast(FP8X4),
                             rhs_scale=tiles[j]["x_scales"][:],
@@ -314,11 +316,13 @@ def tile_hdmodel_pb_t_e_kernel(
         w1_planes = const.tile([P, EXPERTS // PLANES_PER_TILE, H], U8, align_bytes=64)
         w2_planes = const.tile([P, EXPERTS * H_PASSES // PLANES_PER_TILE, D], U8, align_bytes=64)
         vectors = const.tile([P, D], BF16)
+        early_vectors = const.tile([P, D], BF16)
+        nc.vector.memset(early_vectors[:], 0.0)
         nc.vector.memset(vectors[:], 0.0)
-        nc.vector.memset(w1_planes_raw[:].rearrange("p b n -> p (b n)").bitcast(I32), 0)
-        nc.vector.memset(w2_planes[:].rearrange("p b n -> p (b n)").bitcast(I32), 0)
         neg_half = const.tile([P, PAIR], F32)
         nc.vector.memset(neg_half[:], -0.5)
+        nc.vector.memset(w1_planes_raw[:].rearrange("p b n -> p (b n)").bitcast(I32), 0)
+        nc.vector.memset(w2_planes[:].rearrange("p b n -> p (b n)").bitcast(I32), 0)
         ident = const.tile([P, P], F32)
         make_identity(nc, ident[:])
         ident_bf16 = const.tile([P, P], BF16)
@@ -330,22 +334,26 @@ def tile_hdmodel_pb_t_e_kernel(
             in_=ident_bf16[:, TE_ROW : TE_ROW + TASKS].unsqueeze(2).to_broadcast([P, TASKS, B_TILE]),
         )
 
-        nc.scalar.dma_start(out=vectors[TE_ROW : TE_ROW + TASKS, :], in_=task_emb)
+        nc.scalar.dma_start(out=early_vectors[TE_ROW : TE_ROW + TASKS, :], in_=task_emb)
         nc.scalar.dma_start(
-            out=vectors[B1_ROW : B1_ROW + B1_ROWS, :], in_=b1.rearrange("e (c k) -> (e c) k", c=H_PASSES)
+            out=early_vectors[B1_ROW : B1_ROW + B1_ROWS, :], in_=b1.rearrange("e (c k) -> (e c) k", c=H_PASSES)
         )
-        load_rows(0)
+        nc.scalar.dma_start(out=vectors[TE_ROW : TE_ROW + TASKS, :], in_=task_emb)
         for row, vector in ((B2_ROW, b2), (GAIN_ROW, ln_g), (BIAS_ROW, ln_b)):
-            nc.sync.dma_start(out=vectors[row : row + EXPERTS, :], in_=vector)
+            nc.scalar.dma_start(out=vectors[row : row + EXPERTS, :], in_=vector)
+        load_w1_chunk(0, 1)
+        load_rows(0)
+        load_planes(w1_planes_raw, W1_scales, 0)
+        load_w1_chunk(0, 0)
         table_load = const.tile([P, 1], F32)
         nc.scalar.activation(out=table_load[:], in_=neg_half[:, 0:1], func=ACT.Silu)
-        load_w1(0)
         load_rows(1)
         load_rows(2)
         load_w1(1)
         load_w2(0)
+        sort_columns(0, 1)
         vector_psum = psum_h.tile([P, ROWS, 2], F32, name="h_psum")
-        transpose_rows(vector_psum, 0, vectors[:])
+        transpose_rows(vector_psum, 0, early_vectors[:])
         te_cols = const.tile([P, ROWS, PACK], BF16)
         for i in range(PAIR):
             nc.vector.tensor_copy(
@@ -377,10 +385,12 @@ def tile_hdmodel_pb_t_e_kernel(
                 quantise_hidden(j - 1)
             if live(j + 1):
                 quantise_rows(j + 1)
-            if j == 0:
-                sort_columns(1)
             if j == -1:
-                sort_columns(0)
+                sort_plane_columns(0, 0)
+                sort_columns(0, 0)
+            if j == 0:
+                for c in reversed(range(H_PASSES)):
+                    sort_columns(1, c)
             if live(j + 2):
                 add_task_embedding(j + 2)
             if j == -2:
@@ -389,8 +399,12 @@ def tile_hdmodel_pb_t_e_kernel(
                     in_=vector_psum[:, B1_ROW : B1_ROW + B1_ROWS, :],
                 )
                 nc.vector.tensor_copy(out=b1_cols[:], in_=b1_bf16[:])
+                sort_plane_columns(0, 1)
             if j >= 0 and j % PAIRS_PER_EXPERT == 0 and next_expert + 1 < EXPERTS:
-                sort_columns(next_expert + 1)
+                for c in reversed(range(H_PASSES)):
+                    if (next_expert + 1) % PLANES_PER_TILE == 0:
+                        sort_plane_columns((next_expert + 1) // PLANES_PER_TILE, c)
+                    sort_columns(next_expert + 1, c)
             if live(j - 1):
                 second_matmul(j - 1)
             if live(j + 1):

@@ -273,7 +273,7 @@ def tile_hdmodel_pb_t_e_kernel(
             dev_sum = stat_pool.tile([P, PAIR], F32)
             var_eps = stat_pool.tile([P, PAIR], F32)
             rstd = stat_pool.tile([P, PAIR], F32)
-            squares = work.tile([P, D], BF16)
+            squares = work.tile([P, PAIR, D], BF16)
             step = 1 if j == N_PAIRS - 1 else PAIR
             for first in range(0, PAIR, step):
                 cols = slice(first, first + step)
@@ -282,7 +282,7 @@ def tile_hdmodel_pb_t_e_kernel(
                 )
                 for i in range(first, first + step):
                     nc.scalar.activation(
-                        out=squares[:], in_=tiles[j]["r"][:, i, :], func=ACT.Square, bias=neg_mean[:, i : i + 1],
+                        out=squares[:, i, :], in_=tiles[j]["r"][:, i, :], func=ACT.Square, bias=neg_mean[:, i : i + 1],
                         scale=1.0, accum_out=dev_sum[:, i : i + 1],
                     )
                 nc.scalar.activation(
@@ -391,6 +391,11 @@ def tile_hdmodel_pb_t_e_kernel(
             if j == 0:
                 for c in reversed(range(H_PASSES)):
                     sort_columns(1, c)
+            if j >= 0 and j % PAIRS_PER_EXPERT == 1 and next_expert + 1 < EXPERTS:
+                for c in reversed(range(H_PASSES)):
+                    if (next_expert + 1) % PLANES_PER_TILE == 0:
+                        sort_plane_columns((next_expert + 1) // PLANES_PER_TILE, c)
+                    sort_columns(next_expert + 1, c)
             if live(j + 2):
                 add_task_embedding(j + 2)
             if j == -2:
@@ -400,11 +405,6 @@ def tile_hdmodel_pb_t_e_kernel(
                 )
                 nc.vector.tensor_copy(out=b1_cols[:], in_=b1_bf16[:])
                 sort_plane_columns(0, 1)
-            if j >= 0 and j % PAIRS_PER_EXPERT == 0 and next_expert + 1 < EXPERTS:
-                for c in reversed(range(H_PASSES)):
-                    if (next_expert + 1) % PLANES_PER_TILE == 0:
-                        sort_plane_columns((next_expert + 1) // PLANES_PER_TILE, c)
-                    sort_columns(next_expert + 1, c)
             if live(j - 1):
                 second_matmul(j - 1)
             if live(j + 1):
@@ -416,8 +416,8 @@ def tile_hdmodel_pb_t_e_kernel(
                 spread_gain_and_bias(0)
             if live(j):
                 silu(j)
-                interleave_hidden(j)
                 residual_input(j)
+                interleave_hidden(j)
             if live(j - 2):
                 centre_and_gain(j - 2)
             if live(j - 1):

@@ -202,6 +202,8 @@ def tile_hdmodel_pb_t_e_kernel(
                         func=ACT.Silu,
                         bias=b1_cols[:, expert_of(j) * H_PASSES + c, t : t + 1],
                     )
+                    if (c, t) == (H_PASSES - 1, 0) and j >= 2:
+                        inverse_std(j - 2, slice(0, PAIR))
             tiles[j]["h_planes"] = h_planes
 
         def interleave_hidden(j):
@@ -268,31 +270,34 @@ def tile_hdmodel_pb_t_e_kernel(
             tiles[j]["r"] = r
             tiles[j]["r_sum"] = r_sum
 
-        def row_statistics(j):
-            neg_mean = stat_pool.tile([P, PAIR], F32)
-            dev_sum = stat_pool.tile([P, PAIR], F32)
-            var_eps = stat_pool.tile([P, PAIR], F32)
-            rstd = stat_pool.tile([P, PAIR], F32)
+        def sum_deviations(j):
+            for stat in ("neg_mean", "dev_sum", "var_eps", "rstd"):
+                tiles[j][stat] = stat_pool.tile([P, PAIR], F32, name=stat)
             squares = work.tile([P, PAIR, D], BF16)
-            step = 1 if j == N_PAIRS - 1 else PAIR
-            for first in range(0, PAIR, step):
-                cols = slice(first, first + step)
+            for i in range(PAIR):
                 nc.scalar.activation(
-                    out=neg_mean[:, cols], in_=tiles[j]["r_sum"][:, cols], func=ACT.Copy, scale=-1.0 / D
+                    out=tiles[j]["neg_mean"][:, i : i + 1], in_=tiles[j]["r_sum"][:, i : i + 1],
+                    func=ACT.Copy, scale=-1.0 / D,
                 )
-                for i in range(first, first + step):
-                    nc.scalar.activation(
-                        out=squares[:, i, :], in_=tiles[j]["r"][:, i, :], func=ACT.Square, bias=neg_mean[:, i : i + 1],
-                        scale=1.0, accum_out=dev_sum[:, i : i + 1],
-                    )
+            for i in range(PAIR):
                 nc.scalar.activation(
-                    out=var_eps[:, cols], in_=dev_sum[:, cols], func=ACT.Copy, scale=1.0 / D, bias=LN_EPS
+                    out=squares[:, i, :], in_=tiles[j]["r"][:, i, :], func=ACT.Square,
+                    bias=tiles[j]["neg_mean"][:, i : i + 1], scale=1.0,
+                    accum_out=tiles[j]["dev_sum"][:, i : i + 1],
                 )
-                nc.gpsimd.tensor_tensor(
-                    out=rstd[:, cols], in0=var_eps[:, cols], in1=neg_half[:, cols], op=ALU.pow
-                )
-            tiles[j]["neg_mean"] = neg_mean
-            tiles[j]["rstd"] = rstd
+                if j == N_PAIRS - 1:
+                    inverse_std(j, slice(i, i + 1))
+            if j == N_PAIRS - 2:
+                inverse_std(j, slice(0, PAIR))
+
+        def inverse_std(j, cols):
+            nc.scalar.activation(
+                out=tiles[j]["var_eps"][:, cols], in_=tiles[j]["dev_sum"][:, cols], func=ACT.Copy,
+                scale=1.0 / D, bias=LN_EPS,
+            )
+            nc.gpsimd.tensor_tensor(
+                out=tiles[j]["rstd"][:, cols], in0=tiles[j]["var_eps"][:, cols], in1=neg_half[:, cols], op=ALU.pow
+            )
 
         def centre_and_gain(j):
             gained = work.tile([P, PAIR, D], F32)
@@ -427,6 +432,6 @@ def tile_hdmodel_pb_t_e_kernel(
             if j % PAIRS_PER_EXPERT == PAIRS_PER_EXPERT - 1 and 1 <= expert_of(j) < EXPERTS:
                 spread_gain_and_bias(expert_of(j))
             if live(j - 1):
-                row_statistics(j - 1)
+                sum_deviations(j - 1)
             if prepare:
                 expert_constant(next_expert)

from contextlib import ExitStack

import concourse.mybir as mybir
from concourse.masks import make_identity

F32 = mybir.dt.float32
BF16 = mybir.dt.bfloat16
I32 = mybir.dt.int32
U32 = mybir.dt.uint32
U8 = mybir.dt.uint8
FP8X4 = mybir.dt.float8_e4m3fn_x4
ALU = mybir.AluOpType
ACT = mybir.ActivationFunctionType

P = 128
PACK = 4
K_PASS = P * PACK
BATCH, EXPERTS, TASKS, D, H = 32, 8, 16, 512, 1024
LN_EPS = 1e-5

B_TILE = P // TASKS
PAIR = 2
ROWS = PAIR * P
PAIRS_PER_EXPERT = BATCH // (B_TILE * PAIR)
N_PAIRS = EXPERTS * PAIRS_PER_EXPERT
H_PASSES = H // K_PASS
PLANES_PER_TILE = 4
GPSIMD_ROWS = 160
ROWS_AHEAD = 6
W1_AHEAD = 7
W2_AHEAD = 4
TE_ROW = 0
B2_ROW = TE_ROW + TASKS
GAIN_ROW = B2_ROW + EXPERTS
BIAS_ROW = GAIN_ROW + EXPERTS
B1_ROW = TE_ROW + TASKS
B1_ROWS = EXPERTS * H_PASSES

FLOPS = 2 * BATCH * EXPERTS * TASKS * (D * H + H * D)


def tile_hdmodel_pb_t_e_kernel(
    tc, xs_mix, task_emb, W1_words, W1_scales, b1, W2_words, W2_scales, b2, ln_g, ln_b, out
):
    nc = tc.nc
    with ExitStack() as ctx:
        ctx.enter_context(tc.manual_schedule())
        const = ctx.enter_context(tc.tile_pool(name="const", bufs=1))
        expert_pool = ctx.enter_context(tc.tile_pool(name="expert", bufs=6))
        rows_pool = ctx.enter_context(tc.tile_pool(name="rows", bufs=ROWS_AHEAD + 2))
        work = ctx.enter_context(tc.tile_pool(name="work", bufs=3))
        stat_pool = ctx.enter_context(tc.tile_pool(name="stat", bufs=4))
        psum_x = ctx.enter_context(tc.psum_pool(name="psum_x", bufs=1))
        psum_spread = ctx.enter_context(tc.psum_pool(name="psum_spread", bufs=1))
        psum_h = ctx.enter_context(tc.psum_pool(name="psum_h", bufs=4))
        psum_o = ctx.enter_context(tc.psum_pool(name="psum_o", bufs=2))

        experts = {}
        tiles = {}

        def expert_of(j):
            return j // PAIRS_PER_EXPERT

        def dram_rows(tensor, j, i):
            e, pair = divmod(j, PAIRS_PER_EXPERT)
            first = B_TILE * (PAIR * pair + i)
            return tensor[first : first + B_TILE, e].rearrange("b t d -> t b d")

        def load_planes(planes, scales, block):
            first = PLANES_PER_TILE * block
            for quadrant in range(4):
                nc.sync.dma_start(
                    out=planes[32 * quadrant : 32 * quadrant + 16, block, :].bitcast(I32),
                    in_=scales[
                        first : first + PLANES_PER_TILE, 4 * quadrant : 4 * quadrant + 4, :
                    ].bitcast(I32),
                )

        def load_w1_chunk(e, c):
            raw = expert_pool.tile([P, PACK * K_PASS], U8, name="w1_raw_%d" % c, align_bytes=64)
            nc.sync.dma_start(
                out=raw[:].bitcast(I32),
                in_=W1_words[e, :, K_PASS * c : K_PASS * (c + 1), :].rearrange("p n t -> p (n t)").bitcast(I32),
            )
            w1_sorted = expert_pool.tile([P, PACK, P], I32, name="w1_sorted_%d" % c, align_bytes=64)
            experts.setdefault(e, {})["w1_raw", c] = raw
            experts[e]["w1_words", c] = w1_sorted

        def load_w1(e):
            if e % PLANES_PER_TILE == 0:
                load_planes(w1_planes_raw, W1_scales, e // PLANES_PER_TILE)
            for c in reversed(range(H_PASSES)):
                load_w1_chunk(e, c)

        def load_w2(e):
            if (e * H_PASSES) % PLANES_PER_TILE == 0:
                load_planes(w2_planes, W2_scales, e * H_PASSES // PLANES_PER_TILE)
            w2_words = expert_pool.tile([P, H_PASSES, PACK * D], U8, align_bytes=64)
            for c in range(H_PASSES):
                nc.sync.dma_start(
                    out=w2_words[:, c, :].bitcast(I32),
                    in_=W2_words[e * H_PASSES + c].rearrange("p n t -> p (n t)").bitcast(I32),
                )
            experts[e]["w2_words"] = w2_words

        def load_rows(j):
            x_rows = rows_pool.tile([P, PAIR, D], BF16)
            for i in range(PAIR):
                nc.sync.dma_start(out=x_rows[:, i, :], in_=dram_rows(xs_mix, j, i))
            tiles[j] = dict(x_rows=x_rows)

        def one_row(row):
            return ident_bf16[:, row : row + 1].to_broadcast([P, P])

        def spread_gain_and_bias(e):
            gain_bias = psum_spread.tile([P, 2, D], BF16)
            for i, row in enumerate((GAIN_ROW, BIAS_ROW)):
                nc.tensor.matmul(out=gain_bias[:, i, :], lhsT=one_row(row + e), rhs=vectors[:], start=True, stop=True)
            experts[e]["gain"] = gain_bias[:, 0, :]
            experts[e]["bias"] = gain_bias[:, 1, :]

        def expert_constant(e):
            te_b2_psum = psum_o.tile([P, D], F32, name="o_psum")
            nc.tensor.matmul(out=te_b2_psum[:], lhsT=task_of_row[:], rhs=vectors[:], start=True, stop=False)
            nc.tensor.matmul(out=te_b2_psum[:], lhsT=one_row(B2_ROW + e), rhs=vectors[:], start=False, stop=True)
            te_b2 = expert_pool.tile([P, D], F32)
            nc.scalar.copy(out=te_b2[:], in_=te_b2_psum[:])
            experts[e]["te_b2"] = te_b2

        def sort_plane_columns(block, c):
            cols = slice(K_PASS * c, K_PASS * (c + 1))
            nc.vector.tensor_copy(
                out=w1_planes[:, block, cols].rearrange("p (t m) -> p m t", t=PACK),
                in_=w1_planes_raw[:, block, cols].rearrange("p (m t) -> p m t", t=PACK),
            )

        def sort_columns(e, c):
            nc.vector.tensor_copy(
                out=experts[e]["w1_words", c][:].rearrange("p t m -> p m t"),
                in_=experts[e]["w1_raw", c][:].bitcast(I32).rearrange("p (m t) -> p m t", t=PACK),
            )

        def transpose_rows(x_cols, i, x_rows):
            words = x_rows.bitcast(F32)
            for u in range(2):
                nc.tensor.transpose(x_cols[:, P * i : P * (i + 1), u], words[:, u : D // 2 : 2], ident[:])

        def transpose_pair(j):
            x_cols = psum_x.tile([P, ROWS, 2], F32)
            for i in range(PAIR):
                transpose_rows(x_cols, i, tiles[j]["x_rows"][:, i, :])
            tiles[j]["x_cols"] = x_cols

        def add_task_embedding(j):
            x_grouped = work.tile([P, ROWS, PACK], BF16, align_bytes=64)
            nc.vector.tensor_tensor(
                out=x_grouped[:].rearrange("p r t -> p (r t)"),
                in0=tiles[j]["x_cols"][:].rearrange("p r u -> p (r u)").bitcast(BF16),
                in1=te_cols[:].rearrange("p r t -> p (r t)"),
                op=ALU.add,
            )
            tiles[j]["x_grouped"] = x_grouped

        def quantise_rows(j):
            x_codes = work.tile([P, ROWS], U32, align_bytes=64)
            x_scales = work.tile([P, ROWS], U8, align_bytes=64)
            nc.vector.quantize_mx(
                out=x_codes[:].bitcast(FP8X4),
                scales=x_scales[:],
                in_=tiles[j]["x_grouped"][:].rearrange("p r t -> p (r t)"),
            )
            tiles[j]["x_codes"] = x_codes
            tiles[j]["x_scales"] = x_scales

        def first_matmul(j):
            e = expert_of(j)
            block, plane = divmod(e, PLANES_PER_TILE)
            tiles[j]["h_psum"] = {}
            for c in reversed(range(H_PASSES)):
                for half in range(2):
                    h_psum = psum_h.tile([P, 2, ROWS], F32)
                    for t in range(2):
                        first = K_PASS * c + P * (2 * half + t)
                        nc.tensor.matmul_mx(
                            out=h_psum[:, t, :],
                            lhsT=experts[e]["w1_words", c][:, 2 * half + t, :].bitcast(FP8X4),
                            lhsT_scale=w1_planes[4 * plane : P, block, first : first + P],
                            rhs=tiles[j]["x_codes"][:].bitcast(FP8X4),
                            rhs_scale=tiles[j]["x_scales"][:],
                            start=True,
                            stop=True,
                        )
                    tiles[j]["h_psum"][c, half] = h_psum

        def silu(j):
            h_planes = work.tile([P, H_PASSES, PACK, ROWS], BF16, align_bytes=64)
            for c in reversed(range(H_PASSES)):
                for t in range(PACK):
                    nc.scalar.activation(
                        out=h_planes[:, c, t, :],
                        in_=tiles[j]["h_psum"][c, t // 2][:, t % 2, :],
                        func=ACT.Silu,
                        bias=b1_cols[:, expert_of(j) * H_PASSES + c, t : t + 1],
                    )
                    if (c, t) == (H_PASSES - 1, 0) and j >= 2:
                        inverse_std(j - 2, slice(0, PAIR))
            tiles[j]["h_planes"] = h_planes

        def interleave_hidden(j):
            h_grouped = work.tile([P, H_PASSES, ROWS, PACK], BF16, align_bytes=64)
            nc.gpsimd.tensor_scalar(
                out=h_grouped[:, 1, 0:GPSIMD_ROWS],
                in0=tiles[j]["h_planes"][:, 1, :, 0:GPSIMD_ROWS].rearrange("p t r -> p r t"),
                scalar1=1.0, scalar2=0.0, op0=ALU.mult, op1=ALU.add,
            )
            for c, first in ((1, GPSIMD_ROWS), (0, 0)):
                nc.scalar.copy(
                    out=h_grouped[:, c, first:ROWS].rearrange("p (q i) t -> p q t i", i=4),
                    in_=tiles[j]["h_planes"][:, c, :, first:ROWS].rearrange("p t (q i) -> p q t i", i=4),
                )
            tiles[j]["h_grouped"] = h_grouped

        def quantise_hidden(j):
            h_codes = work.tile([P, H_PASSES, ROWS], U32, align_bytes=64)
            h_scales = work.tile([P, H_PASSES, ROWS], U8, align_bytes=64)
            nc.vector.quantize_mx(
                out=h_codes[:].rearrange("p c r -> p (c r)").bitcast(FP8X4),
                scales=h_scales[:].rearrange("p c r -> p (c r)"),
                in_=tiles[j]["h_grouped"][:].rearrange("p c r t -> p (c r t)"),
            )
            tiles[j]["h_codes"] = h_codes
            tiles[j]["h_scales"] = h_scales

        def second_matmul(j):
            e = expert_of(j)
            tiles[j]["o_psum"] = []
            for i in range(PAIR):
                o_psum = psum_o.tile([P, D], F32)
                for c in range(H_PASSES):
                    block, plane = divmod(e * H_PASSES + c, PLANES_PER_TILE)
                    nc.tensor.matmul_mx(
                        out=o_psum[:],
                        lhsT=tiles[j]["h_codes"][:, c, P * i : P * (i + 1)].bitcast(FP8X4),
                        lhsT_scale=tiles[j]["h_scales"][:, c, P * i : P * (i + 1)],
                        rhs=experts[e]["w2_words"][:, c, :].bitcast(FP8X4),
                        rhs_scale=w2_planes[4 * plane : P, block, :],
                        start=(c == 0),
                        stop=(c == H_PASSES - 1),
                    )
                tiles[j]["o_psum"].append(o_psum)

        def residual_input(j):
            resid = work.tile([P, PAIR, D], F32)
            nc.gpsimd.tensor_tensor(
                out=resid[:],
                in0=tiles[j]["x_rows"][:],
                in1=experts[expert_of(j)]["te_b2"][:].unsqueeze(1).to_broadcast([P, PAIR, D]),
                op=ALU.add,
            )
            tiles[j]["resid"] = resid

        def add_residual(j):
            r = work.tile([P, PAIR, D], F32)
            r_sum = stat_pool.tile([P, PAIR], F32)
            for i in range(PAIR):
                nc.vector.scalar_tensor_tensor(
                    out=r[:, i, :], in0=tiles[j]["o_psum"][i][:], scalar=1.0, in1=tiles[j]["resid"][:, i, :],
                    op0=ALU.mult, op1=ALU.add, accum_out=r_sum[:, i : i + 1],
                )
            tiles[j]["r"] = r
            tiles[j]["r_sum"] = r_sum

        def sum_deviations(j):
            for stat in ("neg_mean", "dev_sum", "var_eps", "rstd"):
                tiles[j][stat] = stat_pool.tile([P, PAIR], F32, name=stat)
            squares = work.tile([P, PAIR, D], BF16)
            for i in range(PAIR):
                nc.scalar.activation(
                    out=tiles[j]["neg_mean"][:, i : i + 1], in_=tiles[j]["r_sum"][:, i : i + 1],
                    func=ACT.Copy, scale=-1.0 / D,
                )
            for i in range(PAIR):
                nc.scalar.activation(
                    out=squares[:, i, :], in_=tiles[j]["r"][:, i, :], func=ACT.Square,
                    bias=tiles[j]["neg_mean"][:, i : i + 1], scale=1.0,
                    accum_out=tiles[j]["dev_sum"][:, i : i + 1],
                )
                if j == N_PAIRS - 1:
                    inverse_std(j, slice(i, i + 1))
            if j == N_PAIRS - 2:
                inverse_std(j, slice(0, PAIR))

        def inverse_std(j, cols):
            nc.scalar.activation(
                out=tiles[j]["var_eps"][:, cols], in_=tiles[j]["dev_sum"][:, cols], func=ACT.Copy,
                scale=1.0 / D, bias=LN_EPS,
            )
            nc.gpsimd.tensor_tensor(
                out=tiles[j]["rstd"][:, cols], in0=tiles[j]["var_eps"][:, cols], in1=neg_half[:, cols], op=ALU.pow
            )

        def centre_and_gain(j):
            gained = work.tile([P, PAIR, D], F32)
            for i in range(PAIR):
                nc.vector.scalar_tensor_tensor(
                    out=gained[:, i, :], in0=tiles[j]["r"][:, i, :], scalar=tiles[j]["neg_mean"][:, i : i + 1],
                    in1=experts[expert_of(j)]["gain"], op0=ALU.add, op1=ALU.mult,
                )
            tiles[j]["gained"] = gained

        def scale_bias_and_store(j):
            y = work.tile([P, PAIR, D], F32)
            for i in range(PAIR):
                nc.vector.scalar_tensor_tensor(
                    out=y[:, i, :], in0=tiles[j]["gained"][:, i, :], scalar=tiles[j]["rstd"][:, i : i + 1],
                    in1=experts[expert_of(j)]["bias"], op0=ALU.mult, op1=ALU.add,
                )
                nc.sync.dma_start(out=dram_rows(out, j, i), in_=y[:, i, :])

        w1_planes_raw = const.tile([P, EXPERTS // PLANES_PER_TILE, H], U8, align_bytes=64)
        w1_planes = const.tile([P, EXPERTS // PLANES_PER_TILE, H], U8, align_bytes=64)
        w2_planes = const.tile([P, EXPERTS * H_PASSES // PLANES_PER_TILE, D], U8, align_bytes=64)
        vectors = const.tile([P, D], BF16)
        early_vectors = const.tile([P, D], BF16)
        nc.vector.memset(early_vectors[:], 0.0)
        nc.vector.memset(vectors[:], 0.0)
        neg_half = const.tile([P, PAIR], F32)
        nc.vector.memset(neg_half[:], -0.5)
        nc.vector.memset(w1_planes_raw[:].rearrange("p b n -> p (b n)").bitcast(I32), 0)
        nc.vector.memset(w2_planes[:].rearrange("p b n -> p (b n)").bitcast(I32), 0)
        ident = const.tile([P, P], F32)
        make_identity(nc, ident[:])
        ident_bf16 = const.tile([P, P], BF16)
        make_identity(nc, ident_bf16[:])

        task_of_row = const.tile([P, P], BF16)
        nc.vector.tensor_copy(
            out=task_of_row[:].rearrange("p (k b) -> p k b", k=TASKS),
            in_=ident_bf16[:, TE_ROW : TE_ROW + TASKS].unsqueeze(2).to_broadcast([P, TASKS, B_TILE]),
        )

        nc.scalar.dma_start(out=early_vectors[TE_ROW : TE_ROW + TASKS, :], in_=task_emb)
        nc.scalar.dma_start(
            out=early_vectors[B1_ROW : B1_ROW + B1_ROWS, :], in_=b1.rearrange("e (c k) -> (e c) k", c=H_PASSES)
        )
        nc.scalar.dma_start(out=vectors[TE_ROW : TE_ROW + TASKS, :], in_=task_emb)
        for row, vector in ((B2_ROW, b2), (GAIN_ROW, ln_g), (BIAS_ROW, ln_b)):
            nc.scalar.dma_start(out=vectors[row : row + EXPERTS, :], in_=vector)
        load_w1_chunk(0, 1)
        load_rows(0)
        load_planes(w1_planes_raw, W1_scales, 0)
        load_w1_chunk(0, 0)
        table_load = const.tile([P, 1], F32)
        nc.scalar.activation(out=table_load[:], in_=neg_half[:, 0:1], func=ACT.Silu)
        load_rows(1)
        load_rows(2)
        load_w1(1)
        load_w2(0)
        sort_columns(0, 1)
        vector_psum = psum_h.tile([P, ROWS, 2], F32, name="h_psum")
        transpose_rows(vector_psum, 0, early_vectors[:])
        te_cols = const.tile([P, ROWS, PACK], BF16)
        for i in range(PAIR):
            nc.vector.tensor_copy(
                out=te_cols[:, P * i : P * (i + 1), :].rearrange("p r t -> p (r t)").bitcast(F32).rearrange(
                    "p (k b u) -> p k b u", k=TASKS, u=2
                ),
                in_=vector_psum[:, TE_ROW : TE_ROW + TASKS, :]
                .unsqueeze(2)
                .to_broadcast([P, TASKS, B_TILE, 2]),
            )
        b1_bf16 = const.tile([P, B1_ROWS, PACK], BF16)
        b1_cols = const.tile([P, B1_ROWS, PACK], F32)

        def live(j):
            return 0 <= j < N_PAIRS

        for j in range(-3, N_PAIRS + 2):
            if 3 <= j + ROWS_AHEAD < N_PAIRS:
                load_rows(j + ROWS_AHEAD)
            e, pair = divmod(j + W1_AHEAD, PAIRS_PER_EXPERT)
            if pair == 0 and 2 <= e < EXPERTS:
                load_w1(e)
            e, pair = divmod(j + W2_AHEAD, PAIRS_PER_EXPERT)
            if pair == 0 and 1 <= e < EXPERTS:
                load_w2(e)
            next_expert = expert_of(j) + 1
            prepare = j >= 0 and j % PAIRS_PER_EXPERT == 0 and next_expert < EXPERTS
            if live(j - 1):
                quantise_hidden(j - 1)
            if live(j + 1):
                quantise_rows(j + 1)
            if j == -1:
                sort_plane_columns(0, 0)
                sort_columns(0, 0)
            if j == 0:
                for c in reversed(range(H_PASSES)):
                    sort_columns(1, c)
            if j >= 0 and j % PAIRS_PER_EXPERT == 1 and next_expert + 1 < EXPERTS:
                for c in reversed(range(H_PASSES)):
                    if (next_expert + 1) % PLANES_PER_TILE == 0:
                        sort_plane_columns((next_expert + 1) // PLANES_PER_TILE, c)
                    sort_columns(next_expert + 1, c)
            if live(j + 2):
                add_task_embedding(j + 2)
            if j == -2:
                nc.vector.tensor_copy(
                    out=b1_bf16[:].rearrange("p r t -> p (r t)").bitcast(F32).rearrange("p (r u) -> p r u", u=2),
                    in_=vector_psum[:, B1_ROW : B1_ROW + B1_ROWS, :],
                )
                nc.vector.tensor_copy(out=b1_cols[:], in_=b1_bf16[:])
                sort_plane_columns(0, 1)
            if live(j - 1):
                second_matmul(j - 1)
            if live(j + 1):
                first_matmul(j + 1)
            if live(j + 3):
                transpose_pair(j + 3)
            if j == -3:
                expert_constant(0)
                spread_gain_and_bias(0)
            if live(j):
                silu(j)
                residual_input(j)
                interleave_hidden(j)
            if live(j - 2):
                centre_and_gain(j - 2)
            if live(j - 1):
                add_residual(j - 1)
            if live(j - 2):
                scale_bias_and_store(j - 2)
            if j % PAIRS_PER_EXPERT == PAIRS_PER_EXPERT - 1 and 1 <= expert_of(j) < EXPERTS:
                spread_gain_and_bias(expert_of(j))
            if live(j - 1):
                sum_deviations(j - 1)
            if prepare:
                expert_constant(next_expert)
